import numpy as np
import ml_dtypes


def mxq(x, axis, fmt="e4m3"):
    dtype, down = {"e4m3": (ml_dtypes.float8_e4m3fn, 7), "e5m2": (ml_dtypes.float8_e5m2, 14)}[fmt]
    v = np.moveaxis(np.asarray(x, np.float32).astype(ml_dtypes.bfloat16).astype(np.float64), axis, -1)
    blocks = v.reshape(v.shape[:-1] + (-1, 32))
    amax = np.abs(blocks).max(-1, keepdims=True)
    byte = np.maximum(np.where(amax > 0, np.frexp(amax)[1] - 1 + 127, 0) - down, 1)
    scale = np.exp2(byte - 127.0)
    codes = (blocks / scale).astype(np.float32).astype(dtype).astype(np.float64)
    return np.moveaxis((codes * scale).reshape(v.shape), -1, axis)


WIDE = False


def mx_kscale(k):
    if not WIDE:
        return np.ones(k)
    levels = np.array([30, -30])
    if k % 512:
        return np.exp2(np.random.permutation(np.resize(levels, k // 32))).repeat(32)
    a = np.empty((k // 512, 16))
    for p in range(k // 512):
        a[p, :8] = np.random.permutation(np.resize(levels, 8))
        for g in range(8):
            far = levels[np.abs(levels - a[p, g]) >= 10]
            a[p, g + 8] = far[np.random.randint(len(far))]
    return np.exp2(a.ravel()).repeat(32)


BF16 = ml_dtypes.bfloat16


def bf(x):
    return np.asarray(x, np.float32).astype(BF16)


def f64(x):
    return np.asarray(x).astype(np.float64)


B, S, H, NH, NKV, HD, WINDOW, C, TAPS = 2, 1024, 1024, 8, 4, 128, 512, 512, 2
THETA = 100000.0
QW, KW = NH * HD, NKV * HD


def softmax(v):
    e = np.exp(v - v.max(-1, keepdims=True))
    return e / e.sum(-1, keepdims=True)


def rope(x, cos, sin):
    d2 = x.shape[-1] // 2
    x1, x2 = x[..., :d2], x[..., d2:]
    c = cos[None, :, None, :]
    s = sin[None, :, None, :]
    return np.concatenate([x1 * c - x2 * s, x2 * c + x1 * s], axis=-1)


def causal_conv2(x, w):
    x_prev = np.concatenate([np.zeros_like(x[:, :1]), x[:, :-1]], axis=1)
    return w[None, None, :, 0:1] * x_prev + w[None, None, :, 1:2] * x


def setup_inputs():
    s = mx_kscale(H)
    cs = np.concatenate([np.ones(QW + KW), 3.0 * np.ones(KW)])
    return {"hidden": bf(np.random.standard_normal((B, S, H)) * s),
            "W_pack": bf(np.random.standard_normal((H, QW + KW + KW)) * cs / np.sqrt(H) / s[:, None]),
            "conv_k": bf(softmax(np.random.standard_normal((NKV, TAPS)))),
            "conv_v": bf(softmax(np.random.standard_normal((NKV, TAPS))))}


def reference(hidden, W_pack, conv_k, conv_v):
    qkv = mxq(f64(hidden), 2, "e5m2") @ mxq(f64(W_pack), 0, "e4m3")
    q = qkv[..., :QW].reshape(B, S, NH, HD)
    k = qkv[..., QW:QW + KW].reshape(B, S, NKV, HD)
    v = qkv[..., QW + KW:].reshape(B, S, NKV, HD)
    inv_freq = 1.0 / THETA ** (np.arange(0, HD, 2) / HD)
    freqs = np.outer(np.arange(S), inv_freq)
    cos, sin = np.cos(freqs), np.sin(freqs)
    q = rope(q, cos, sin)
    k = rope(k, cos, sin)
    k = causal_conv2(k, f64(conv_k))
    v = causal_conv2(v, f64(conv_v))
    return q, k, v

@@ -1,0 +1,409 @@
+import math
+from contextlib import ExitStack
+
+import concourse.mybir as mybir
+from concourse.masks import make_identity
+
+F32 = mybir.dt.float32
+BF16 = mybir.dt.bfloat16
+I32 = mybir.dt.int32
+U32 = mybir.dt.uint32
+U8 = mybir.dt.uint8
+E5M2X4 = mybir.dt.float8_e5m2_x4
+E4M3X4 = mybir.dt.float8_e4m3fn_x4
+ALU = mybir.AluOpType
+ACT = mybir.ActivationFunctionType
+
+P = 128
+SEQ = 1024
+K = 1024
+TILES = 16
+PASSES = 2
+K_PASS = 512
+BANK = 512
+HEAD = 128
+HALF = 64
+HEADS_PER_BANK = 4
+THETA = 100000.0
+Q0, Q1, KEYS, VALUES = 0, 1, 2, 3
+
+FLOPS = 2 * 2048 * 1024 * 2048
+
+
+def tile_baichuanattention_pa_kernel(tc, hidden, W_pack, conv_k, conv_v, out_0, out_1, out_2):
+    nc = tc.nc
+    hid = hidden.rearrange("b (pp j) k -> (b pp) j k", j=TILES)
+    q_out = out_0.rearrange("b (pp j) h d -> (b pp) j (h d)", j=TILES)
+    k_out = out_1.rearrange("b (pp j) h d -> (b pp) j (h d)", j=TILES)
+    v_out = out_2.rearrange("b (pp j) h d -> (b pp) j (h d)", j=TILES)
+
+    with ExitStack() as ctx:
+        keep = ctx.enter_context(tc.tile_pool(name="keep", bufs=1))
+        work = ctx.enter_context(tc.tile_pool(name="work", bufs=2))
+        psum = ctx.enter_context(tc.psum_pool(name="psum", bufs=8))
+        ctx.enter_context(tc.manual_schedule())
+
+        h_codes = keep.tile([P, PASSES, TILES * P], U32, align_bytes=64)
+        h_scales = keep.tile([P, PASSES, TILES * P], U8, align_bytes=64)
+        w_codes = keep.tile([P, PASSES, 4 * BANK], U32, align_bytes=64)
+        w_scales = keep.tile([P, PASSES, 4 * BANK], U8, align_bytes=64)
+
+        def new_bank():
+            bank = psum.tile([P, BANK], F32, tag="bank", name="bank")
+            return bank
+
+        w_raw = {}
+        h_raw = {}
+
+        def load_w(group, g):
+            raw = work.tile([P, 4, BANK], BF16, tag="w_raw", name="w_raw", bufs=6)
+            rows = W_pack[g * K_PASS : (g + 1) * K_PASS, group * BANK : (group + 1) * BANK]
+            nc.sync.dma_start(out=raw[:], in_=rows.rearrange("(p t) n -> p t n", t=4))
+            w_raw[group, g] = raw
+
+        def load_h(m):
+            raw = work.tile([P, 2, K], BF16, tag="h_raw", name="h_raw", bufs=6)
+            lo = TILES - 2 - 2 * m
+            nc.sync.dma_start(out=raw[:], in_=hid[:, lo : lo + 2, :])
+            h_raw[m] = raw
+
+        load_w(Q0, 0)
+        load_h(0)
+        load_w(Q0, 1)
+        load_h(1)
+        load_h(2)
+        load_w(KEYS, 0)
+        load_h(3)
+        load_w(KEYS, 1)
+        load_h(4)
+        load_w(Q1, 0)
+        load_h(5)
+        load_w(Q1, 1)
+
+        eye2 = keep.tile([P, 2 * P], F32)
+        ident = eye2[:, 0:P]
+        swap = eye2[:, HALF : HALF + P]
+        pos_t = keep.tile([P, TILES], F32)
+        nc.gpsimd.iota(pos_t[0:64, :], [[1, TILES]], base=0, channel_multiplier=TILES, allow_small_or_imprecise_dtypes=True)
+        nc.gpsimd.iota(pos_t[64:128, :], [[1, TILES]], base=0, channel_multiplier=TILES, allow_small_or_imprecise_dtypes=True)
+        make_identity(nc, eye2[:, 0:P])
+        make_identity(nc, eye2[:, P : 2 * P])
+        pos_c = keep.tile([P, TILES, 64], F32)
+        nc.gpsimd.iota(pos_c[:], [[1, TILES], [TILES, 64]], base=0, channel_multiplier=0, allow_small_or_imprecise_dtypes=True)
+        shift = keep.tile([P, P], F32)
+        nc.gpsimd.memset(shift[:], 0.0)
+        nc.gpsimd.affine_select(
+            out=shift[:], in_=shift[:], compare_op=ALU.not_equal, fill=1.0, base=1, pattern=[[-1, P]], channel_multiplier=1
+        )
+        nc.gpsimd.memset(shift[:, 64:65], 0.0)
+
+        ones = keep.tile([P, 1], F32)
+        nc.vector.memset(ones[:], 1.0)
+        sign = keep.tile([P, 1], F32)
+        nc.vector.memset(sign[0:64, :], 1.0)
+        nc.vector.memset(sign[64:128, :], -1.0)
+        coarse = keep.tile([P, 8], F32)
+        fine = keep.tile([P, 8], F32)
+        for a in range(8):
+            nc.vector.tensor_scalar(
+                out=coarse[:, a : a + 1], in0=ones[:], scalar1=THETA ** (-8 * a / HALF) / (2 * math.pi), scalar2=None, op0=ALU.mult
+            )
+            nc.vector.tensor_scalar(out=fine[:, a : a + 1], in0=ones[:], scalar1=THETA ** (-a / HALF), scalar2=None, op0=ALU.mult)
+        freq = keep.tile([P, 2, 8, 8], F32)
+        nc.vector.tensor_tensor(
+            out=freq[:],
+            in0=coarse[:].unsqueeze(1).unsqueeze(3).to_broadcast([P, 2, 8, 8]),
+            in1=fine[:].unsqueeze(1).unsqueeze(1).to_broadcast([P, 2, 8, 8]),
+            op=ALU.mult,
+        )
+        freq_row = freq[:].rearrange("p d a b -> p (d a b)")
+
+        def sin_cos(frac, sin, cos):
+            nc.scalar.activation(out=sin, in_=frac, func=ACT.Sin, scale=2 * math.pi)
+            mag = work.tile([P, SEQ], F32, tag="turns", name="mag")
+            nc.scalar.activation(out=mag[:], in_=frac, func=ACT.Abs)
+            nc.scalar.activation(out=cos, in_=mag[:], func=ACT.Sin, scale=-2 * math.pi, bias=math.pi / 2)
+
+        sin_t = keep.tile([P, TILES, HALF], F32)
+        cos_t = keep.tile([P, TILES, HALF], F32)
+        sin_c = keep.tile([P, TILES, 64], F32)
+        cos_c = keep.tile([P, TILES, 64], F32)
+        frac = keep.tile([P, SEQ], F32)
+        whole = keep.tile([P, SEQ], I32)
+
+        turns = work.tile([P, SEQ], F32, tag="turns", name="turns")
+        nc.vector.tensor_tensor(
+            out=turns[:].rearrange("p (j i) -> p j i", i=HALF),
+            in0=pos_t[:].unsqueeze(2).to_broadcast([P, TILES, HALF]),
+            in1=freq_row[:, 0:HALF].unsqueeze(1).to_broadcast([P, TILES, HALF]),
+            op=ALU.mult,
+        )
+        nc.vector.tensor_copy(out=whole[:], in_=turns[:])
+        nc.vector.tensor_tensor(out=frac[:], in0=turns[:], in1=whole[:], op=ALU.subtract)
+        sin_cos(frac[:], sin_t[:].rearrange("p j i -> p (j i)"), cos_t[:].rearrange("p j i -> p (j i)"))
+
+        w_grouped = {}
+
+        def interleave_w(copy, group, g, lo, hi):
+            if (group, g) not in w_grouped:
+                grouped = work.tile([P, BANK, 4], BF16, tag="w_grouped", name="w_grouped", align_bytes=64)
+                w_grouped[group, g] = grouped
+            copy(
+                out=w_grouped[group, g][:, lo:hi, :].rearrange("p (c i) t -> p c t i", i=4),
+                in_=w_raw[group, g][:, :, lo:hi].rearrange("p t (c i) -> p c t i", i=4),
+            )
+
+        def quantize_w(group, g):
+            cols = slice(group * BANK, (group + 1) * BANK)
+            nc.vector.quantize_mx(
+                out=w_codes[:, g, cols].bitcast(E4M3X4),
+                scales=w_scales[:, g, cols],
+                in_=w_grouped[group, g][:].rearrange("p n t -> p (n t)"),
+            )
+
+        h_grouped = {}
+
+        def transpose_h(m):
+            grouped = work.tile([P, PASSES, 2, 4 * P], BF16, tag="h_grouped", name="h_grouped", bufs=3, align_bytes=64)
+            h_grouped[m] = grouped
+            banks = []
+            for jj in (1, 0):
+                words = h_raw[m][:, jj, :].bitcast(F32)
+                bank = new_bank()
+                for g in range(PASSES):
+                    for u in range(2):
+                        col = (2 * g + u) * P
+                        nc.tensor.transpose(bank[:, col : col + P], words[:, 256 * g + u : 256 * (g + 1) : 2], ident)
+                banks.append((jj, bank))
+            return banks
+
+        def evacuate_h(m, banks):
+            for jj, bank in banks:
+                nc.scalar.copy(
+                    out=h_grouped[m][:, :, jj, :].bitcast(F32).rearrange("p g (r u) -> p g r u", u=2),
+                    in_=bank[:].rearrange("p (g u r) -> p g r u", g=PASSES, u=2),
+                )
+
+        def quantize_h(m):
+            lo = (TILES - 2 - 2 * m) * P
+            for g in range(PASSES):
+                nc.vector.quantize_mx(
+                    out=h_codes[:, g, lo : lo + 2 * P].bitcast(E5M2X4),
+                    scales=h_scales[:, g, lo : lo + 2 * P],
+                    in_=h_grouped[m][:, g, :, :].rearrange("p j c -> p (j c)"),
+                )
+
+        def project_tokens(j, group):
+            bank = new_bank()
+            tok = slice(j * P, (j + 1) * P)
+            cols = slice(group * BANK, (group + 1) * BANK)
+            for g in range(PASSES):
+                nc.tensor.matmul_mx(
+                    out=bank[:],
+                    lhsT=h_codes[:, g, tok].bitcast(E5M2X4),
+                    lhsT_scale=h_scales[:, g, tok],
+                    rhs=w_codes[:, g, cols].bitcast(E4M3X4),
+                    rhs_scale=w_scales[:, g, cols],
+                    start=(g == 0),
+                    stop=(g == PASSES - 1),
+                )
+            return bank
+
+        def project_key_channels(quad, h):
+            bank = new_bank()
+            tok = slice(quad * BANK, (quad + 1) * BANK)
+            cols = slice(KEYS * BANK + h * HEAD, KEYS * BANK + (h + 1) * HEAD)
+            for g in range(PASSES):
+                nc.tensor.matmul_mx(
+                    out=bank[:],
+                    lhsT=w_codes[:, g, cols].bitcast(E4M3X4),
+                    lhsT_scale=w_scales[:, g, cols],
+                    rhs=h_codes[:, g, tok].bitcast(E5M2X4),
+                    rhs_scale=h_scales[:, g, tok],
+                    start=(g == 0),
+                    stop=(g == PASSES - 1),
+                )
+            return bank
+
+        def rope_q(j, group, bank):
+            direct = work.tile([P, BANK], F32, tag="q_direct", name="q_direct", bufs=8)
+            crossed = work.tile([P, HEADS_PER_BANK, 2, HALF], F32, tag="q_crossed", name="q_crossed", bufs=3)
+            nc.vector.tensor_tensor(
+                out=direct[:].rearrange("p (a i) -> p a i", i=HALF),
+                in0=bank[:].rearrange("p (a i) -> p a i", i=HALF),
+                in1=cos_t[:, j, :].unsqueeze(1).to_broadcast([P, 8, HALF]),
+                op=ALU.mult,
+            )
+            x = bank[:].rearrange("p (h d i) -> p h d i", d=2, i=HALF)
+            sin = sin_t[:, j, :].unsqueeze(1).to_broadcast([P, HEADS_PER_BANK, HALF])
+            nc.vector.tensor_tensor(out=crossed[:, :, 1, :], in0=x[:, :, 0, :], in1=sin, op=ALU.mult)
+            nc.vector.scalar_tensor_tensor(
+                out=crossed[:, :, 0, :], in0=x[:, :, 1, :], scalar=-1.0, in1=sin, op0=ALU.mult, op1=ALU.mult
+            )
+            nc.gpsimd.tensor_tensor(
+                out=direct[:], in0=direct[:], in1=crossed[:].rearrange("p h d i -> p (h d i)"), op=ALU.add
+            )
+            nc.sync.dma_start(out=q_out[:, j, group * BANK : (group + 1) * BANK], in_=direct[:])
+
+        key_parts = {}
+
+        def rope_key_products(quad, h, bank):
+            parts = work.tile([P, 2, BANK], F32, tag="key_parts", name="key_parts", bufs=8)
+            key_parts[quad, h] = parts
+            x = bank[:].rearrange("p (j b t) -> p j b t", b=2, t=64)
+            for part, table in ((0, cos_c), (1, sin_c)):
+                nc.vector.tensor_tensor(
+                    out=parts[:, part, :].rearrange("p (j b t) -> p j b t", b=2, t=64),
+                    in0=x,
+                    in1=table[:, 4 * quad : 4 * quad + 4, :].unsqueeze(2).to_broadcast([P, 4, 2, 64]),
+                    op=ALU.mult,
+                )
+
+        def rope_key_sums(j):
+            bank = new_bank()
+            quad, jj = divmod(j, 4)
+            for h in range(HEADS_PER_BANK):
+                parts = key_parts[quad, h]
+                out = bank[:, h * HEAD : (h + 1) * HEAD]
+                tok = slice(jj * P, (jj + 1) * P)
+                nc.tensor.matmul(out, lhsT=parts[:, 0, tok], rhs=ident, is_transpose=True, start=True, stop=False)
+                nc.tensor.matmul(out, lhsT=parts[:, 1, tok], rhs=swap, is_transpose=True, start=False, stop=True)
+            return bank
+
+        def scale_heads(out, bank, taps, tap):
+            for h in range(HEADS_PER_BANK):
+                cols = slice(h * HEAD, (h + 1) * HEAD)
+                nc.scalar.activation(out=out[:, cols], in_=bank[:, cols], func=ACT.Copy, scale=taps[:, 2 * h + tap : 2 * h + tap + 1])
+
+        def add_scaled_heads(acc, bank, taps, tap):
+            for h in range(HEADS_PER_BANK):
+                cols = slice(h * HEAD, (h + 1) * HEAD)
+                nc.vector.scalar_tensor_tensor(
+                    out=acc[:, cols],
+                    in0=bank[:, cols],
+                    scalar=taps[:, 2 * h + tap : 2 * h + tap + 1],
+                    in1=acc[:, cols],
+                    op0=ALU.mult,
+                    op1=ALU.add,
+                )
+
+        interleave_w(nc.vector.tensor_copy, Q0, 0, 0, BANK)
+        banks0 = transpose_h(0)
+        evacuate_h(0, banks0)
+        interleave_w(nc.scalar.copy, Q0, 1, 0, 192)
+        quantize_w(Q0, 0)
+        interleave_w(nc.vector.tensor_copy, Q0, 1, 192, BANK)
+        quantize_h(0)
+        quantize_w(Q0, 1)
+        banks1 = transpose_h(1)
+        evacuate_h(1, banks1)
+
+        load_h(6)
+        load_w(VALUES, 0)
+        load_h(7)
+        load_w(VALUES, 1)
+        taps_k16 = keep.tile([P, 8], BF16)
+        taps_v16 = keep.tile([P, 8], BF16)
+        nc.sync.dma_start(out=taps_k16[:], in_=conv_k.rearrange("h t -> (h t)").partition_broadcast(P))
+        nc.sync.dma_start(out=taps_v16[:], in_=conv_v.rearrange("h t -> (h t)").partition_broadcast(P))
+        taps_k = keep.tile([P, 8], F32)
+        taps_v = keep.tile([P, 8], F32)
+
+        freq_col = keep.tile([P, 1], F32)
+
+        w_plan = {0: (KEYS, 0), 1: (KEYS, 1), 4: (Q1, 0), 5: (Q1, 1), 6: (VALUES, 0), 7: (VALUES, 1)}
+        for m in range(8):
+            hi = TILES - 1 - 2 * m
+            bank_hi = project_tokens(hi, Q0)
+            bank_lo = project_tokens(hi - 1, Q0)
+            if m >= 4:
+                bank_k = project_key_channels(3, m - 4)
+            if m == 0:
+                freq_bank = new_bank()
+                nc.tensor.transpose(freq_bank[:, 0:P], freq_row, ident)
+                nc.scalar.activation(out=freq_col[:], in_=freq_bank[:, 0:1], func=ACT.Copy, scale=sign[:])
+            if m + 2 < 8:
+                banks = transpose_h(m + 2)
+            rope_q(hi, Q0, bank_hi)
+            if m + 1 < 8:
+                quantize_h(m + 1)
+            if m - 1 in w_plan:
+                quantize_w(*w_plan[m - 1])
+            if m == 1:
+                nc.vector.tensor_scalar(
+                    out=whole[:], in0=pos_c[:].rearrange("p j t -> p (j t)"), scalar1=freq_col[:], scalar2=None, op0=ALU.mult
+                )
+            if m + 2 < 8:
+                evacuate_h(m + 2, banks)
+            if m in w_plan:
+                interleave_w(nc.scalar.copy, w_plan[m][0], w_plan[m][1], 0, BANK)
+            rope_q(hi - 1, Q0, bank_lo)
+            if m == 1:
+                nc.vector.scalar_tensor_tensor(
+                    out=frac[:],
+                    in0=pos_c[:].rearrange("p j t -> p (j t)"),
+                    scalar=freq_col[:],
+                    in1=whole[:],
+                    op0=ALU.mult,
+                    op1=ALU.subtract,
+                )
+            if m == 2:
+                sin_cos(frac[:], sin_c[:].rearrange("p j t -> p (j t)"), cos_c[:].rearrange("p j t -> p (j t)"))
+                nc.scalar.copy(out=taps_k[:], in_=taps_k16[:])
+                nc.scalar.copy(out=taps_v[:], in_=taps_v16[:])
+            if m >= 4:
+                rope_key_products(3, m - 4, bank_k)
+        quantize_w(VALUES, 1)
+
+        def conv_tile(tag):
+            part = work.tile([P, BANK], F32, tag=tag, name=tag, bufs=4)
+            return part
+
+        k_acc = {}
+        v_acc = {}
+        wrap_k = keep.tile([P, BANK], F32)
+        wrap_v = keep.tile([P, BANK], F32)
+        for j in range(TILES - 1, -1, -1):
+            unit = TILES - 1 - j + 4
+            bank_kt = rope_key_sums(j)
+            bank_q = project_tokens(j, Q1)
+            bank_v = project_tokens(j, VALUES)
+            if unit < TILES:
+                quad, h = 3 - unit // 4, unit % 4
+                bank_k = project_key_channels(quad, h)
+            rope_q(j, Q1, bank_q)
+            if j > 0:
+                v_acc[j] = conv_tile("v_acc")
+                scale_heads(v_acc[j], bank_v, taps_v, 1)
+            if j == TILES - 1:
+                last_v = conv_tile("prev")
+                scale_heads(last_v, bank_v, taps_v, 0)
+            if unit < TILES:
+                rope_key_products(quad, h, bank_k)
+            if j > 0:
+                k_acc[j] = conv_tile("k_acc")
+                scale_heads(k_acc[j], bank_kt, taps_k, 1)
+            if j < TILES - 1:
+                add_scaled_heads(v_acc[j + 1], bank_v, taps_v, 0)
+                nc.sync.dma_start(out=v_out[:, j + 1, :], in_=v_acc[j + 1][:])
+            if j == TILES - 1:
+                last_k = conv_tile("prev")
+                scale_heads(last_k, bank_kt, taps_k, 0)
+            elif unit < TILES:
+                prev = conv_tile("prev")
+                scale_heads(prev, bank_kt, taps_k, 0)
+                nc.gpsimd.tensor_tensor(out=k_acc[j + 1][:], in0=k_acc[j + 1][:], in1=prev[:], op=ALU.add)
+                nc.sync.dma_start(out=k_out[:, j + 1, :], in_=k_acc[j + 1][:])
+            else:
+                add_scaled_heads(k_acc[j + 1], bank_kt, taps_k, 0)
+                nc.sync.dma_start(out=k_out[:, j + 1, :], in_=k_acc[j + 1][:])
+            if j == TILES - 2:
+                for wrap, last in ((wrap_v, last_v), (wrap_k, last_k)):
+                    bank = new_bank()
+                    nc.tensor.matmul(bank[:], lhsT=shift[:], rhs=last[:], start=True, stop=True)
+                    nc.scalar.copy(out=wrap[:], in_=bank[:])
+            if j == 0:
+                add_scaled_heads(wrap_v, bank_v, taps_v, 1)
+                nc.sync.dma_start(out=v_out[:, 0, :], in_=wrap_v[:])
+                add_scaled_heads(wrap_k, bank_kt, taps_k, 1)
+                nc.sync.dma_start(out=k_out[:, 0, :], in_=wrap_k[:])

@@ -56,46 +56,42 @@ def tile_baichuanattention_pa_kernel(tc, hidden, W_pack, conv_k, conv_v, out_0, 
         h_raw = {}
 
         def load_w(group, g):
-            raw = work.tile([P, 4, BANK], BF16, tag="w_raw", name="w_raw", bufs=6)
+            raw = work.tile([P, 4, BANK], BF16, tag="w_raw", name="w_raw", bufs=4)
             rows = W_pack[g * K_PASS : (g + 1) * K_PASS, group * BANK : (group + 1) * BANK]
             nc.sync.dma_start(out=raw[:], in_=rows.rearrange("(p t) n -> p t n", t=4))
             w_raw[group, g] = raw
 
-        def load_h(m):
-            raw = work.tile([P, 2, K], BF16, tag="h_raw", name="h_raw", bufs=6)
-            lo = TILES - 2 - 2 * m
-            nc.sync.dma_start(out=raw[:], in_=hid[:, lo : lo + 2, :])
-            h_raw[m] = raw
+        def load_h(m, lo, hi):
+            if m not in h_raw:
+                raw = work.tile([P, 2, K], BF16, tag="h_raw", name="h_raw", bufs=4)
+                h_raw[m] = raw
+            first = TILES - 2 - 2 * m
+            nc.sync.dma_start(out=h_raw[m][:, lo:hi, :], in_=hid[:, first + lo : first + hi, :])
 
         load_w(Q0, 0)
-        load_h(0)
+        load_h(0, 1, 2)
         load_w(Q0, 1)
-        load_h(1)
-        load_h(2)
+        load_h(0, 0, 1)
+        load_h(1, 0, 2)
+        load_h(2, 0, 2)
         load_w(KEYS, 0)
-        load_h(3)
+        load_h(3, 0, 2)
         load_w(KEYS, 1)
-        load_h(4)
-        load_w(Q1, 0)
-        load_h(5)
-        load_w(Q1, 1)
 
-        eye2 = keep.tile([P, 2 * P], F32)
-        ident = eye2[:, 0:P]
-        swap = eye2[:, HALF : HALF + P]
+        eye2 = keep.tile([P, 2, P], F32)
+        eye_row = eye2[:].rearrange("p d n -> p (d n)")
+        ident = eye_row[:, 0:P]
+        swap = eye_row[:, HALF : HALF + P]
         pos_t = keep.tile([P, TILES], F32)
         nc.gpsimd.iota(pos_t[0:64, :], [[1, TILES]], base=0, channel_multiplier=TILES, allow_small_or_imprecise_dtypes=True)
         nc.gpsimd.iota(pos_t[64:128, :], [[1, TILES]], base=0, channel_multiplier=TILES, allow_small_or_imprecise_dtypes=True)
-        make_identity(nc, eye2[:, 0:P])
-        make_identity(nc, eye2[:, P : 2 * P])
+        nc.gpsimd.memset(eye_row, 0.0)
+        nc.gpsimd.affine_select(
+            out=eye2[:], in_=eye2[:], compare_op=ALU.not_equal, fill=1.0, base=0, pattern=[[0, 2], [-1, P]], channel_multiplier=1
+        )
         pos_c = keep.tile([P, TILES, 64], F32)
         nc.gpsimd.iota(pos_c[:], [[1, TILES], [TILES, 64]], base=0, channel_multiplier=0, allow_small_or_imprecise_dtypes=True)
-        shift = keep.tile([P, P], F32)
-        nc.gpsimd.memset(shift[:], 0.0)
-        nc.gpsimd.affine_select(
-            out=shift[:], in_=shift[:], compare_op=ALU.not_equal, fill=1.0, base=1, pattern=[[-1, P]], channel_multiplier=1
-        )
-        nc.gpsimd.memset(shift[:, 64:65], 0.0)
+        pos_c_row = pos_c[:].rearrange("p j t -> p (j t)")
 
         ones = keep.tile([P, 1], F32)
         nc.vector.memset(ones[:], 1.0)
@@ -118,29 +114,33 @@ def tile_baichuanattention_pa_kernel(tc, hidden, W_pack, conv_k, conv_v, out_0, 
         )
         freq_row = freq[:].rearrange("p d a b -> p (d a b)")
 
-        def sin_cos(frac, sin, cos):
-            nc.scalar.activation(out=sin, in_=frac, func=ACT.Sin, scale=2 * math.pi)
-            mag = work.tile([P, SEQ], F32, tag="turns", name="mag")
-            nc.scalar.activation(out=mag[:], in_=frac, func=ACT.Abs)
-            nc.scalar.activation(out=cos, in_=mag[:], func=ACT.Sin, scale=-2 * math.pi, bias=math.pi / 2)
-
         sin_t = keep.tile([P, TILES, HALF], F32)
         cos_t = keep.tile([P, TILES, HALF], F32)
         sin_c = keep.tile([P, TILES, 64], F32)
         cos_c = keep.tile([P, TILES, 64], F32)
-        frac = keep.tile([P, SEQ], F32)
-        whole = keep.tile([P, SEQ], I32)
+        frac = keep.tile([P, TILES, 64], F32)
+        whole = keep.tile([P, TILES, 64], U32)
+        frac_row = frac[:].rearrange("p j i -> p (j i)")
+        whole_row = whole[:].rearrange("p j i -> p (j i)")
 
-        turns = work.tile([P, SEQ], F32, tag="turns", name="turns")
-        nc.vector.tensor_tensor(
-            out=turns[:].rearrange("p (j i) -> p j i", i=HALF),
-            in0=pos_t[:].unsqueeze(2).to_broadcast([P, TILES, HALF]),
-            in1=freq_row[:, 0:HALF].unsqueeze(1).to_broadcast([P, TILES, HALF]),
-            op=ALU.mult,
-        )
-        nc.vector.tensor_copy(out=whole[:], in_=turns[:])
-        nc.vector.tensor_tensor(out=frac[:], in0=turns[:], in1=whole[:], op=ALU.subtract)
-        sin_cos(frac[:], sin_t[:].rearrange("p j i -> p (j i)"), cos_t[:].rearrange("p j i -> p (j i)"))
+        def sin_cos(sin, cos, lo, hi):
+            nc.scalar.activation(out=sin[:, lo:hi, :], in_=frac[:, lo:hi, :], func=ACT.Sin, scale=2 * math.pi)
+            nc.scalar.activation(out=cos[:, lo:hi, :], in_=frac[:, lo:hi, :], func=ACT.Abs)
+            nc.scalar.activation(out=cos[:, lo:hi, :], in_=cos[:, lo:hi, :], func=ACT.Sin, scale=-2 * math.pi, bias=math.pi / 2)
+
+        def turns_t(lo, hi):
+            nc.vector.tensor_tensor(
+                out=frac[:, lo:hi, :],
+                in0=pos_t[:, lo:hi].unsqueeze(2).to_broadcast([P, hi - lo, HALF]),
+                in1=freq_row[:, 0:HALF].unsqueeze(1).to_broadcast([P, hi - lo, HALF]),
+                op=ALU.mult,
+            )
+
+        def whole_t(lo, hi):
+            nc.vector.tensor_copy(out=whole[:, lo:hi, :].bitcast(I32), in_=frac[:, lo:hi, :])
+
+        def frac_t(lo, hi):
+            nc.vector.tensor_tensor(out=frac[:, lo:hi, :], in0=frac[:, lo:hi, :], in1=whole[:, lo:hi, :].bitcast(I32), op=ALU.subtract)
 
         w_grouped = {}
 
@@ -163,34 +163,32 @@ def tile_baichuanattention_pa_kernel(tc, hidden, W_pack, conv_k, conv_v, out_0, 
 
         h_grouped = {}
 
-        def transpose_h(m):
-            grouped = work.tile([P, PASSES, 2, 4 * P], BF16, tag="h_grouped", name="h_grouped", bufs=3, align_bytes=64)
-            h_grouped[m] = grouped
-            banks = []
-            for jj in (1, 0):
-                words = h_raw[m][:, jj, :].bitcast(F32)
-                bank = new_bank()
-                for g in range(PASSES):
-                    for u in range(2):
-                        col = (2 * g + u) * P
-                        nc.tensor.transpose(bank[:, col : col + P], words[:, 256 * g + u : 256 * (g + 1) : 2], ident)
-                banks.append((jj, bank))
-            return banks
+        def transpose_h(m, jj):
+            if m not in h_grouped:
+                grouped = work.tile([P, PASSES, 2, 4 * P], BF16, tag="h_grouped", name="h_grouped", bufs=3, align_bytes=64)
+                h_grouped[m] = grouped
+            words = h_raw[m][:, jj, :].bitcast(F32)
+            bank = new_bank()
+            for g in range(PASSES):
+                for u in range(2):
+                    col = (2 * g + u) * P
+                    nc.tensor.transpose(bank[:, col : col + P], words[:, 256 * g + u : 256 * (g + 1) : 2], ident)
+            return bank
 
-        def evacuate_h(m, banks):
-            for jj, bank in banks:
-                nc.scalar.copy(
-                    out=h_grouped[m][:, :, jj, :].bitcast(F32).rearrange("p g (r u) -> p g r u", u=2),
-                    in_=bank[:].rearrange("p (g u r) -> p g r u", g=PASSES, u=2),
-                )
+        def evacuate_h(copy, m, jj, bank):
+            copy(
+                out=h_grouped[m][:, :, jj, :].bitcast(F32).rearrange("p g (r u) -> p g r u", u=2),
+                in_=bank[:].rearrange("p (g u r) -> p g r u", g=PASSES, u=2),
+            )
 
-        def quantize_h(m):
-            lo = (TILES - 2 - 2 * m) * P
+        def quantize_h(m, lo, hi):
+            first = TILES - 2 - 2 * m
+            tok = slice((first + lo) * P, (first + hi) * P)
             for g in range(PASSES):
                 nc.vector.quantize_mx(
-                    out=h_codes[:, g, lo : lo + 2 * P].bitcast(E5M2X4),
-                    scales=h_scales[:, g, lo : lo + 2 * P],
-                    in_=h_grouped[m][:, g, :, :].rearrange("p j c -> p (j c)"),
+                    out=h_codes[:, g, tok].bitcast(E5M2X4),
+                    scales=h_scales[:, g, tok],
+                    in_=h_grouped[m][:, g, lo:hi, :].rearrange("p j c -> p (j c)"),
                 )
 
         def project_tokens(j, group):
@@ -225,8 +223,25 @@ def tile_baichuanattention_pa_kernel(tc, hidden, W_pack, conv_k, conv_v, out_0, 
                 )
             return bank
 
-        def rope_q(j, group, bank):
-            direct = work.tile([P, BANK], F32, tag="q_direct", name="q_direct", bufs=8)
+        def project_value_head(quad, h):
+            bank = new_bank()
+            cols = slice(VALUES * BANK + h * HEAD, VALUES * BANK + (h + 1) * HEAD)
+            for jj in range(4):
+                tok = slice((4 * quad + jj) * P, (4 * quad + jj + 1) * P)
+                for g in range(PASSES):
+                    nc.tensor.matmul_mx(
+                        out=bank[:, jj * HEAD : (jj + 1) * HEAD],
+                        lhsT=h_codes[:, g, tok].bitcast(E5M2X4),
+                        lhsT_scale=h_scales[:, g, tok],
+                        rhs=w_codes[:, g, cols].bitcast(E4M3X4),
+                        rhs_scale=w_scales[:, g, cols],
+                        start=(g == 0),
+                        stop=(g == PASSES - 1),
+                    )
+            return bank
+
+        def q_first(j, bank):
+            direct = work.tile([P, BANK], F32, tag="q_direct", name="q_direct", bufs=6)
             crossed = work.tile([P, HEADS_PER_BANK, 2, HALF], F32, tag="q_crossed", name="q_crossed", bufs=3)
             nc.vector.tensor_tensor(
                 out=direct[:].rearrange("p (a i) -> p a i", i=HALF),
@@ -237,19 +252,23 @@ def tile_baichuanattention_pa_kernel(tc, hidden, W_pack, conv_k, conv_v, out_0, 
             x = bank[:].rearrange("p (h d i) -> p h d i", d=2, i=HALF)
             sin = sin_t[:, j, :].unsqueeze(1).to_broadcast([P, HEADS_PER_BANK, HALF])
             nc.vector.tensor_tensor(out=crossed[:, :, 1, :], in0=x[:, :, 0, :], in1=sin, op=ALU.mult)
+            return direct, crossed
+
+        def q_second(j, group, bank, direct, crossed, adder):
+            x = bank[:].rearrange("p (h d i) -> p h d i", d=2, i=HALF)
+            sin = sin_t[:, j, :].unsqueeze(1).to_broadcast([P, HEADS_PER_BANK, HALF])
             nc.vector.scalar_tensor_tensor(
                 out=crossed[:, :, 0, :], in0=x[:, :, 1, :], scalar=-1.0, in1=sin, op0=ALU.mult, op1=ALU.mult
             )
-            nc.gpsimd.tensor_tensor(
-                out=direct[:], in0=direct[:], in1=crossed[:].rearrange("p h d i -> p (h d i)"), op=ALU.add
-            )
+            adder.tensor_tensor(out=direct[:], in0=direct[:], in1=crossed[:].rearrange("p h d i -> p (h d i)"), op=ALU.add)
             nc.sync.dma_start(out=q_out[:, j, group * BANK : (group + 1) * BANK], in_=direct[:])
 
-        key_parts = {}
+        def rope_q(j, group, bank, adder):
+            direct, crossed = q_first(j, bank)
+            q_second(j, group, bank, direct, crossed, adder)
 
-        def rope_key_products(quad, h, bank):
-            parts = work.tile([P, 2, BANK], F32, tag="key_parts", name="key_parts", bufs=8)
-            key_parts[quad, h] = parts
+        def rope_key_products(quad, bank):
+            parts = work.tile([P, 2, BANK], F32, tag="key_parts", name="key_parts", bufs=3)
             x = bank[:].rearrange("p (j b t) -> p j b t", b=2, t=64)
             for part, table in ((0, cos_c), (1, sin_c)):
                 nc.vector.tensor_tensor(
@@ -258,152 +277,187 @@ def tile_baichuanattention_pa_kernel(tc, hidden, W_pack, conv_k, conv_v, out_0, 
                     in1=table[:, 4 * quad : 4 * quad + 4, :].unsqueeze(2).to_broadcast([P, 4, 2, 64]),
                     op=ALU.mult,
                 )
+            return parts
 
-        def rope_key_sums(j):
+        def rope_key_sums(parts):
             bank = new_bank()
-            quad, jj = divmod(j, 4)
-            for h in range(HEADS_PER_BANK):
-                parts = key_parts[quad, h]
-                out = bank[:, h * HEAD : (h + 1) * HEAD]
+            for jj in range(4):
                 tok = slice(jj * P, (jj + 1) * P)
-                nc.tensor.matmul(out, lhsT=parts[:, 0, tok], rhs=ident, is_transpose=True, start=True, stop=False)
-                nc.tensor.matmul(out, lhsT=parts[:, 1, tok], rhs=swap, is_transpose=True, start=False, stop=True)
+                nc.tensor.matmul(bank[:, tok], lhsT=parts[:, 0, tok], rhs=ident, is_transpose=True, start=True, stop=False)
+                nc.tensor.matmul(bank[:, tok], lhsT=parts[:, 1, tok], rhs=swap, is_transpose=True, start=False, stop=True)
             return bank
 
-        def scale_heads(out, bank, taps, tap):
-            for h in range(HEADS_PER_BANK):
-                cols = slice(h * HEAD, (h + 1) * HEAD)
-                nc.scalar.activation(out=out[:, cols], in_=bank[:, cols], func=ACT.Copy, scale=taps[:, 2 * h + tap : 2 * h + tap + 1])
-
-        def add_scaled_heads(acc, bank, taps, tap):
-            for h in range(HEADS_PER_BANK):
-                cols = slice(h * HEAD, (h + 1) * HEAD)
-                nc.vector.scalar_tensor_tensor(
-                    out=acc[:, cols],
-                    in0=bank[:, cols],
-                    scalar=taps[:, 2 * h + tap : 2 * h + tap + 1],
-                    in1=acc[:, cols],
-                    op0=ALU.mult,
-                    op1=ALU.add,
-                )
-
-        interleave_w(nc.vector.tensor_copy, Q0, 0, 0, BANK)
-        banks0 = transpose_h(0)
-        evacuate_h(0, banks0)
-        interleave_w(nc.scalar.copy, Q0, 1, 0, 192)
-        quantize_w(Q0, 0)
-        interleave_w(nc.vector.tensor_copy, Q0, 1, 192, BANK)
-        quantize_h(0)
-        quantize_w(Q0, 1)
-        banks1 = transpose_h(1)
-        evacuate_h(1, banks1)
-
-        load_h(6)
-        load_w(VALUES, 0)
-        load_h(7)
-        load_w(VALUES, 1)
+        k_stage = keep.tile([P, TILES + 1, BANK], F32)
+        v_stage = keep.tile([P, TILES + 1, BANK], F32)
         taps_k16 = keep.tile([P, 8], BF16)
         taps_v16 = keep.tile([P, 8], BF16)
-        nc.sync.dma_start(out=taps_k16[:], in_=conv_k.rearrange("h t -> (h t)").partition_broadcast(P))
-        nc.sync.dma_start(out=taps_v16[:], in_=conv_v.rearrange("h t -> (h t)").partition_broadcast(P))
         taps_k = keep.tile([P, 8], F32)
         taps_v = keep.tile([P, 8], F32)
+        shift = keep.tile([P, P], F32)
 
+        def convolve(stage, taps, out, unit, bank, on_pool):
+            quad, h = 3 - unit // 4, unit % 4
+            x = bank[:].rearrange("p (j c) -> p j c", c=HEAD)
+            cols = slice(h * HEAD, (h + 1) * HEAD)
+            w_prev, w_own = taps[:, 2 * h : 2 * h + 1], taps[:, 2 * h + 1 : 2 * h + 2]
+            lo = 1 if quad == 0 else 0
+            n = 3 if quad == 3 else 4
+            later = stage[:, 4 * quad + 1 : 4 * quad + 1 + n, cols]
+            nc.scalar.activation(out=stage[:, 4 * quad + lo : 4 * quad + 4, cols], in_=x[:, lo:4, :], func=ACT.Copy, scale=w_own)
+            if quad == 3:
+                nc.scalar.activation(out=stage[:, TILES, cols], in_=x[:, 3, :], func=ACT.Copy, scale=w_prev)
+            if on_pool:
+                prev = work.tile([P, 5, HEAD], F32, tag="prev", name="prev", bufs=3)
+                nc.scalar.activation(out=prev[:, 1 : 1 + n, :], in_=x[:, 0:n, :], func=ACT.Copy, scale=w_prev)
+                if quad == 0:
+                    nc.scalar.activation(out=prev[:, 0, :], in_=x[:, 0, :], func=ACT.Copy, scale=w_own)
+                target = stage[:, 4 * quad + 1 - lo : 4 * quad + 1 + n, cols]
+                nc.gpsimd.tensor_tensor(out=target, in0=target, in1=prev[:, 1 - lo : 1 + n, :], op=ALU.add)
+            else:
+                nc.vector.scalar_tensor_tensor(out=later, in0=x[:, 0:n, :], scalar=w_prev, in1=later, op0=ALU.mult, op1=ALU.add)
+                if quad == 0:
+                    first = stage[:, 0, cols]
+                    nc.vector.scalar_tensor_tensor(out=first, in0=x[:, 0, :], scalar=w_own, in1=first, op0=ALU.mult, op1=ALU.add)
+            if quad == 0:
+                nc.sync.dma_start(out=out[:, 0:5, cols], in_=stage[:, 0:5, cols])
+            elif h == HEADS_PER_BANK - 1:
+                nc.sync.dma_start(out=out[:, 4 * quad + 1 : 4 * quad + 1 + n, :], in_=stage[:, 4 * quad + 1 : 4 * quad + 1 + n, :])
+
+        def shift_last_tile(stage):
+            wrap = new_bank()
+            nc.tensor.matmul(wrap[:], lhsT=shift[:], rhs=stage[:, TILES, :], start=True, stop=True)
+            nc.scalar.copy(out=stage[:, 0, :], in_=wrap[:])
+
+        FIRST = 14
+        turns_t(FIRST, TILES)
+        whole_t(FIRST, TILES)
+        frac_t(FIRST, TILES)
+        sin_cos(sin_t, cos_t, FIRST, TILES)
+        turns_t(0, FIRST)
+        interleave_w(nc.scalar.copy, Q0, 0, 0, BANK)
+        whole_t(0, FIRST)
+        evacuate_h(nc.scalar.copy, 0, 1, transpose_h(0, 1))
+        interleave_w(nc.vector.tensor_copy, Q0, 1, 0, BANK)
+        evacuate_h(nc.scalar.copy, 0, 0, transpose_h(0, 0))
+        quantize_w(Q0, 0)
+        quantize_h(0, 1, 2)
+        quantize_w(Q0, 1)
+        quantize_h(0, 0, 1)
+        for jj in (1, 0):
+            evacuate_h(nc.scalar.copy, 1, jj, transpose_h(1, jj))
+        first_banks = [project_tokens(15, Q0), project_tokens(14, Q0)]
+        frac_t(0, FIRST)
+        sin_cos(sin_t, cos_t, 10, FIRST)
+        quantize_h(1, 0, 2)
+        for jj in (1, 0):
+            evacuate_h(nc.scalar.copy, 2, jj, transpose_h(2, jj))
         freq_col = keep.tile([P, 1], F32)
+        freq_bank = new_bank()
+        nc.tensor.transpose(freq_bank[:, 0:P], freq_row, ident)
+        nc.scalar.activation(out=freq_col[:], in_=freq_bank[:, 0:1], func=ACT.Copy, scale=sign[:])
+        sin_cos(sin_t, cos_t, 0, 10)
 
-        w_plan = {0: (KEYS, 0), 1: (KEYS, 1), 4: (Q1, 0), 5: (Q1, 1), 6: (VALUES, 0), 7: (VALUES, 1)}
-        for m in range(8):
+        w_plan = {0: (KEYS, 0), 1: (KEYS, 1), 2: (VALUES, 0), 3: (VALUES, 1), 4: (Q1, 0), 5: (Q1, 1)}
+        load_h(4, 0, 2)
+        load_w(VALUES, 0)
+        load_h(5, 0, 2)
+        load_w(VALUES, 1)
+        load_h(6, 0, 2)
+        nc.sync.dma_start(out=taps_v16[:], in_=conv_v.rearrange("h t -> (h t)").partition_broadcast(P))
+        nc.sync.dma_start(out=taps_k16[:], in_=conv_k.rearrange("h t -> (h t)").partition_broadcast(P))
+
+        EARLY, K_FIRST, V_FIRST = 7, 3, 5
+        value_unit = 0
+        key_unit = 0
+        parts = None
+        for m in range(EARLY):
             hi = TILES - 1 - 2 * m
-            bank_hi = project_tokens(hi, Q0)
-            bank_lo = project_tokens(hi - 1, Q0)
-            if m >= 4:
-                bank_k = project_key_channels(3, m - 4)
+            with_k = m >= K_FIRST
+            with_v = m >= V_FIRST
             if m == 0:
-                freq_bank = new_bank()
-                nc.tensor.transpose(freq_bank[:, 0:P], freq_row, ident)
-                nc.scalar.activation(out=freq_col[:], in_=freq_bank[:, 0:1], func=ACT.Copy, scale=sign[:])
+                bank_hi, bank_lo = first_banks
+            else:
+                bank_hi = project_tokens(hi, Q0)
+            if with_k:
+                bank_k = project_key_channels(3 - key_unit // 4, key_unit % 4)
+            if m > 0:
+                bank_lo = project_tokens(hi - 1, Q0)
+            if with_v:
+                bank_v = project_value_head(3 - value_unit // 4, value_unit % 4)
+            summed = parts
+            if summed is not None:
+                bank_kt = rope_key_sums(summed)
+            if m + 3 < 8:
+                h_banks = [transpose_h(m + 3, 1), transpose_h(m + 3, 0)]
+            rope_q(hi, Q0, bank_hi, nc.gpsimd)
+            if summed is not None:
+                convolve(k_stage, taps_k, k_out, key_unit - 1, bank_kt, True)
+            if with_k:
+                parts = rope_key_products(3 - key_unit // 4, bank_k)
+                key_unit += 1
+            direct, crossed = q_first(hi - 1, bank_lo)
+            if with_v:
+                convolve(v_stage, taps_v, v_out, value_unit, bank_v, False)
+                value_unit += 1
+            if m < 3:
+                evacuate_h(nc.vector.tensor_copy, m + 3, 1, h_banks[0])
             if m + 2 < 8:
-                banks = transpose_h(m + 2)
-            rope_q(hi, Q0, bank_hi)
-            if m + 1 < 8:
-                quantize_h(m + 1)
+                quantize_h(m + 2, 0, 2)
             if m - 1 in w_plan:
                 quantize_w(*w_plan[m - 1])
-            if m == 1:
-                nc.vector.tensor_scalar(
-                    out=whole[:], in0=pos_c[:].rearrange("p j t -> p (j t)"), scalar1=freq_col[:], scalar2=None, op0=ALU.mult
-                )
-            if m + 2 < 8:
-                evacuate_h(m + 2, banks)
-            if m in w_plan:
-                interleave_w(nc.scalar.copy, w_plan[m][0], w_plan[m][1], 0, BANK)
-            rope_q(hi - 1, Q0, bank_lo)
+            if m == 1 - 1:
+                nc.vector.tensor_scalar(out=whole_row.bitcast(I32), in0=pos_c_row, scalar1=freq_col[:], scalar2=None, op0=ALU.mult)
             if m == 1:
                 nc.vector.scalar_tensor_tensor(
-                    out=frac[:],
-                    in0=pos_c[:].rearrange("p j t -> p (j t)"),
-                    scalar=freq_col[:],
-                    in1=whole[:],
-                    op0=ALU.mult,
-                    op1=ALU.subtract,
+                    out=frac_row, in0=pos_c_row, scalar=freq_col[:], in1=whole_row.bitcast(I32), op0=ALU.mult, op1=ALU.subtract
                 )
+            q_second(hi - 1, Q0, bank_lo, direct, crossed, nc.gpsimd)
+            if m + 3 < 8:
+                if m >= 3:
+                    evacuate_h(nc.scalar.copy, m + 3, 1, h_banks[0])
+                evacuate_h(nc.scalar.copy, m + 3, 0, h_banks[1])
             if m == 2:
-                sin_cos(frac[:], sin_c[:].rearrange("p j t -> p (j t)"), cos_c[:].rearrange("p j t -> p (j t)"))
-                nc.scalar.copy(out=taps_k[:], in_=taps_k16[:])
+                sin_cos(sin_c, cos_c, 0, TILES)
+            if m in w_plan:
+                interleave_w(nc.scalar.copy, w_plan[m][0], w_plan[m][1], 0, BANK)
+            if m == 0:
+                load_h(7, 0, 2)
+                load_w(Q1, 0)
+            if m == 1:
+                load_w(Q1, 1)
                 nc.scalar.copy(out=taps_v[:], in_=taps_v16[:])
-            if m >= 4:
-                rope_key_products(3, m - 4, bank_k)
-        quantize_w(VALUES, 1)
+                nc.scalar.copy(out=taps_k[:], in_=taps_k16[:])
 
-        def conv_tile(tag):
-            part = work.tile([P, BANK], F32, tag=tag, name=tag, bufs=4)
-            return part
+        if EARLY - 1 in w_plan:
+            quantize_w(*w_plan[EARLY - 1])
 
-        k_acc = {}
-        v_acc = {}
-        wrap_k = keep.tile([P, BANK], F32)
-        wrap_v = keep.tile([P, BANK], F32)
-        for j in range(TILES - 1, -1, -1):
-            unit = TILES - 1 - j + 4
-            bank_kt = rope_key_sums(j)
-            bank_q = project_tokens(j, Q1)
-            bank_v = project_tokens(j, VALUES)
-            if unit < TILES:
-                quad, h = 3 - unit // 4, unit % 4
-                bank_k = project_key_channels(quad, h)
-            rope_q(j, Q1, bank_q)
-            if j > 0:
-                v_acc[j] = conv_tile("v_acc")
-                scale_heads(v_acc[j], bank_v, taps_v, 1)
-            if j == TILES - 1:
-                last_v = conv_tile("prev")
-                scale_heads(last_v, bank_v, taps_v, 0)
-            if unit < TILES:
-                rope_key_products(quad, h, bank_k)
-            if j > 0:
-                k_acc[j] = conv_tile("k_acc")
-                scale_heads(k_acc[j], bank_kt, taps_k, 1)
-            if j < TILES - 1:
-                add_scaled_heads(v_acc[j + 1], bank_v, taps_v, 0)
-                nc.sync.dma_start(out=v_out[:, j + 1, :], in_=v_acc[j + 1][:])
-            if j == TILES - 1:
-                last_k = conv_tile("prev")
-                scale_heads(last_k, bank_kt, taps_k, 0)
-            elif unit < TILES:
-                prev = conv_tile("prev")
-                scale_heads(prev, bank_kt, taps_k, 0)
-                nc.gpsimd.tensor_tensor(out=k_acc[j + 1][:], in0=k_acc[j + 1][:], in1=prev[:], op=ALU.add)
-                nc.sync.dma_start(out=k_out[:, j + 1, :], in_=k_acc[j + 1][:])
-            else:
-                add_scaled_heads(k_acc[j + 1], bank_kt, taps_k, 0)
-                nc.sync.dma_start(out=k_out[:, j + 1, :], in_=k_acc[j + 1][:])
-            if j == TILES - 2:
-                for wrap, last in ((wrap_v, last_v), (wrap_k, last_k)):
-                    bank = new_bank()
-                    nc.tensor.matmul(bank[:], lhsT=shift[:], rhs=last[:], start=True, stop=True)
-                    nc.scalar.copy(out=wrap[:], in_=bank[:])
-            if j == 0:
-                add_scaled_heads(wrap_v, bank_v, taps_v, 1)
-                nc.sync.dma_start(out=v_out[:, 0, :], in_=wrap_v[:])
-                add_scaled_heads(wrap_k, bank_kt, taps_k, 1)
-                nc.sync.dma_start(out=k_out[:, 0, :], in_=wrap_k[:])
+        nc.gpsimd.memset(shift[:], 0.0)
+        nc.gpsimd.affine_select(
+            out=shift[:], in_=shift[:], compare_op=ALU.not_equal, fill=1.0, base=1, pattern=[[-1, P]], channel_multiplier=1
+        )
+        nc.gpsimd.memset(shift[:, 64:65], 0.0)
+        q_jobs = [(j, Q0) for j in range(TILES - 1 - 2 * EARLY, -1, -1)] + [(j, Q1) for j in range(TILES - 1, -1, -1)]
+        for step, (j, group) in enumerate(q_jobs):
+            with_k = key_unit < TILES
+            with_v = value_unit < TILES and True
+            bank_q = project_tokens(j, group)
+            if with_k:
+                bank_k = project_key_channels(3 - key_unit // 4, key_unit % 4)
+            if with_v:
+                bank_v = project_value_head(3 - value_unit // 4, value_unit % 4)
+            summed = parts
+            if summed is not None:
+                bank_kt = rope_key_sums(summed)
+            rope_q(j, group, bank_q, nc.gpsimd if step < len(q_jobs) - 0 else nc.vector)
+            parts = rope_key_products(3 - key_unit // 4, bank_k) if with_k else None
+            if with_v:
+                convolve(v_stage, taps_v, v_out, value_unit, bank_v, False)
+                value_unit += 1
+            if summed is not None:
+                convolve(k_stage, taps_k, k_out, key_unit - 1, bank_kt, True)
+            if with_k:
+                key_unit += 1
+            if step == 6:
+                shift_last_tile(v_stage)
+            if step == 2:
+                shift_last_tile(k_stage)

@@ -2,7 +2,6 @@ import math
 from contextlib import ExitStack
 
 import concourse.mybir as mybir
-from concourse.masks import make_identity
 
 F32 = mybir.dt.float32
 BF16 = mybir.dt.bfloat16
@@ -15,27 +14,46 @@ ALU = mybir.AluOpType
 ACT = mybir.ActivationFunctionType
 
 P = 128
-SEQ = 1024
 K = 1024
-TILES = 16
+SLOTS = 8
+QUAD = 4
+QUADS = 4
+PAIRS = 8
 PASSES = 2
 K_PASS = 512
 BANK = 512
 HEAD = 128
 HALF = 64
-HEADS_PER_BANK = 4
+HEADS = 4
 THETA = 100000.0
 Q0, Q1, KEYS, VALUES = 0, 1, 2, 3
 
+SHIFT_SPLIT = 112
+
 FLOPS = 2 * 2048 * 1024 * 2048
+
+POOL_V = (0, 4)
+K_FIRST, V_FIRST = 3, 7
+TABLES_AT = {2: 4, 7: 0}
+W_SPLIT = 448
+HEAD_SPLIT = 128
+W_LAG = 1
+LOWER_AT = 2
 
 
 def tile_baichuanattention_pa_kernel(tc, hidden, W_pack, conv_k, conv_v, out_0, out_1, out_2):
     nc = tc.nc
-    hid = hidden.rearrange("b (pp j) k -> (b pp) j k", j=TILES)
-    q_out = out_0.rearrange("b (pp j) h d -> (b pp) j (h d)", j=TILES)
-    k_out = out_1.rearrange("b (pp j) h d -> (b pp) j (h d)", j=TILES)
-    v_out = out_2.rearrange("b (pp j) h d -> (b pp) j (h d)", j=TILES)
+    hid = hidden.rearrange("b (p j) k -> b p j k", j=SLOTS)
+    q_out = out_0.rearrange("b (p j) h d -> b p j (h d)", j=SLOTS)
+    k_out = out_1.rearrange("b (p j) h d -> b p j (h d)", j=SLOTS)
+    v_out = out_2.rearrange("b (p j) h d -> b p j (h d)", j=SLOTS)
+
+    def quad_place(quad):
+        return quad % 2, QUAD * (1 - quad // 2)
+
+    def pair_place(pair):
+        batch, first = quad_place(pair // 2)
+        return batch, first + 2 * (pair % 2)
 
     with ExitStack() as ctx:
         keep = ctx.enter_context(tc.tile_pool(name="keep", bufs=1))
@@ -43,10 +61,14 @@ def tile_baichuanattention_pa_kernel(tc, hidden, W_pack, conv_k, conv_v, out_0, 
         psum = ctx.enter_context(tc.psum_pool(name="psum", bufs=8))
         ctx.enter_context(tc.manual_schedule())
 
-        h_codes = keep.tile([P, PASSES, TILES * P], U32, align_bytes=64)
-        h_scales = keep.tile([P, PASSES, TILES * P], U8, align_bytes=64)
+        h_codes = keep.tile([P, PASSES, 16 * P], U32, align_bytes=64)
+        h_scales = keep.tile([P, PASSES, 16 * P], U8, align_bytes=64)
         w_codes = keep.tile([P, PASSES, 4 * BANK], U32, align_bytes=64)
         w_scales = keep.tile([P, PASSES, 4 * BANK], U8, align_bytes=64)
+        k_stage = keep.tile([P, 2, SLOTS, BANK], F32)
+        v_stage = keep.tile([P, 2, SLOTS, BANK], F32)
+        k_last = keep.tile([P, 2, BANK], F32)
+        v_last = keep.tile([P, 2, BANK], F32)
 
         def new_bank():
             bank = psum.tile([P, BANK], F32, tag="bank", name="bank")
@@ -61,17 +83,17 @@ def tile_baichuanattention_pa_kernel(tc, hidden, W_pack, conv_k, conv_v, out_0, 
             nc.sync.dma_start(out=raw[:], in_=rows.rearrange("(p t) n -> p t n", t=4))
             w_raw[group, g] = raw
 
-        def load_h(m, lo, hi):
-            if m not in h_raw:
+        def load_h(pair, lo, hi):
+            if pair not in h_raw:
                 raw = work.tile([P, 2, K], BF16, tag="h_raw", name="h_raw", bufs=4)
-                h_raw[m] = raw
-            first = TILES - 2 - 2 * m
-            nc.sync.dma_start(out=h_raw[m][:, lo:hi, :], in_=hid[:, first + lo : first + hi, :])
+                h_raw[pair] = raw
+            batch, first = pair_place(pair)
+            nc.sync.dma_start(out=h_raw[pair][:, lo:hi, :], in_=hid[batch, :, first + lo : first + hi, :])
 
         load_w(Q0, 0)
-        load_h(0, 1, 2)
-        load_w(Q0, 1)
         load_h(0, 0, 1)
+        load_w(Q0, 1)
+        load_h(0, 1, 2)
         load_h(1, 0, 2)
         load_h(2, 0, 2)
         load_w(KEYS, 0)
@@ -82,22 +104,21 @@ def tile_baichuanattention_pa_kernel(tc, hidden, W_pack, conv_k, conv_v, out_0, 
         eye_row = eye2[:].rearrange("p d n -> p (d n)")
         ident = eye_row[:, 0:P]
         swap = eye_row[:, HALF : HALF + P]
-        pos_t = keep.tile([P, TILES], F32)
-        nc.gpsimd.iota(pos_t[0:64, :], [[1, TILES]], base=0, channel_multiplier=TILES, allow_small_or_imprecise_dtypes=True)
-        nc.gpsimd.iota(pos_t[64:128, :], [[1, TILES]], base=0, channel_multiplier=TILES, allow_small_or_imprecise_dtypes=True)
+        position = keep.tile([P, SLOTS], F32)
+        nc.gpsimd.iota(position[:], [[1, SLOTS]], base=0, channel_multiplier=SLOTS, allow_small_or_imprecise_dtypes=True)
         nc.gpsimd.memset(eye_row, 0.0)
         nc.gpsimd.affine_select(
-            out=eye2[:], in_=eye2[:], compare_op=ALU.not_equal, fill=1.0, base=0, pattern=[[0, 2], [-1, P]], channel_multiplier=1
+            out=eye2[:],
+            in_=eye2[:],
+            compare_op=ALU.not_equal,
+            fill=1.0,
+            base=0,
+            pattern=[[0, 2], [-1, P]],
+            channel_multiplier=1,
         )
-        pos_c = keep.tile([P, TILES, 64], F32)
-        nc.gpsimd.iota(pos_c[:], [[1, TILES], [TILES, 64]], base=0, channel_multiplier=0, allow_small_or_imprecise_dtypes=True)
-        pos_c_row = pos_c[:].rearrange("p j t -> p (j t)")
 
         ones = keep.tile([P, 1], F32)
         nc.vector.memset(ones[:], 1.0)
-        sign = keep.tile([P, 1], F32)
-        nc.vector.memset(sign[0:64, :], 1.0)
-        nc.vector.memset(sign[64:128, :], -1.0)
         coarse = keep.tile([P, 8], F32)
         fine = keep.tile([P, 8], F32)
         for a in range(8):
@@ -105,48 +126,60 @@ def tile_baichuanattention_pa_kernel(tc, hidden, W_pack, conv_k, conv_v, out_0, 
                 out=coarse[:, a : a + 1], in0=ones[:], scalar1=THETA ** (-8 * a / HALF) / (2 * math.pi), scalar2=None, op0=ALU.mult
             )
             nc.vector.tensor_scalar(out=fine[:, a : a + 1], in0=ones[:], scalar1=THETA ** (-a / HALF), scalar2=None, op0=ALU.mult)
-        freq = keep.tile([P, 2, 8, 8], F32)
+        freq = keep.tile([P, 8, 8], F32)
         nc.vector.tensor_tensor(
             out=freq[:],
-            in0=coarse[:].unsqueeze(1).unsqueeze(3).to_broadcast([P, 2, 8, 8]),
-            in1=fine[:].unsqueeze(1).unsqueeze(1).to_broadcast([P, 2, 8, 8]),
+            in0=coarse[:].unsqueeze(2).to_broadcast([P, 8, 8]),
+            in1=fine[:].unsqueeze(1).to_broadcast([P, 8, 8]),
             op=ALU.mult,
         )
-        freq_row = freq[:].rearrange("p d a b -> p (d a b)")
+        turns = v_stage[:, 1, 1, :].rearrange("p (j i) -> p j i", i=HALF)
+        whole = v_stage[:, 1, 2, :].bitcast(I32).rearrange("p (j i) -> p j i", i=HALF)
+        size = v_stage[:, 1, 3, :].rearrange("p (j i) -> p j i", i=HALF)
+        nc.vector.tensor_tensor(
+            out=turns,
+            in0=position[:].unsqueeze(2).to_broadcast([P, SLOTS, HALF]),
+            in1=freq[:].rearrange("p a b -> p (a b)").unsqueeze(1).to_broadcast([P, SLOTS, HALF]),
+            op=ALU.mult,
+        )
+        nc.vector.tensor_copy(out=whole, in_=turns)
 
-        sin_t = keep.tile([P, TILES, HALF], F32)
-        cos_t = keep.tile([P, TILES, HALF], F32)
-        sin_c = keep.tile([P, TILES, 64], F32)
-        cos_c = keep.tile([P, TILES, 64], F32)
-        frac = keep.tile([P, TILES, 64], F32)
-        whole = keep.tile([P, TILES, 64], U32)
-        frac_row = frac[:].rearrange("p j i -> p (j i)")
-        whole_row = whole[:].rearrange("p j i -> p (j i)")
+        rot_t = keep.tile([P, SLOTS, 5, HALF], F32)
+        rot_c = keep.tile([P, 2, SLOTS * P], F32)
 
-        def sin_cos(sin, cos, lo, hi):
-            nc.scalar.activation(out=sin[:, lo:hi, :], in_=frac[:, lo:hi, :], func=ACT.Sin, scale=2 * math.pi)
-            nc.scalar.activation(out=cos[:, lo:hi, :], in_=frac[:, lo:hi, :], func=ACT.Abs)
-            nc.scalar.activation(out=cos[:, lo:hi, :], in_=cos[:, lo:hi, :], func=ACT.Sin, scale=-2 * math.pi, bias=math.pi / 2)
-
-        def turns_t(lo, hi):
-            nc.vector.tensor_tensor(
-                out=frac[:, lo:hi, :],
-                in0=pos_t[:, lo:hi].unsqueeze(2).to_broadcast([P, hi - lo, HALF]),
-                in1=freq_row[:, 0:HALF].unsqueeze(1).to_broadcast([P, hi - lo, HALF]),
-                op=ALU.mult,
+        def token_tables(lo, hi):
+            nc.scalar.activation(out=rot_t[:, lo:hi, 1, :], in_=turns[:, lo:hi, :], func=ACT.Sin, scale=-2 * math.pi)
+            nc.scalar.activation(out=size[:, lo:hi, :], in_=turns[:, lo:hi, :], func=ACT.Abs)
+            nc.scalar.activation(out=rot_t[:, lo:hi, 2, :], in_=turns[:, lo:hi, :], func=ACT.Sin, scale=2 * math.pi)
+            nc.scalar.activation(
+                out=rot_t[:, lo:hi, 0:4:3, :],
+                in_=size[:, lo:hi, :].unsqueeze(2).to_broadcast([P, hi - lo, 2, HALF]),
+                func=ACT.Sin,
+                scale=-2 * math.pi,
+                bias=math.pi / 2,
             )
 
-        def whole_t(lo, hi):
-            nc.vector.tensor_copy(out=whole[:, lo:hi, :].bitcast(I32), in_=frac[:, lo:hi, :])
+        def second_cosine(first):
+            nc.scalar.copy(out=rot_t[:, first : first + QUAD, 4, :], in_=rot_t[:, first : first + QUAD, 0, :])
 
-        def frac_t(lo, hi):
-            nc.vector.tensor_tensor(out=frac[:, lo:hi, :], in0=frac[:, lo:hi, :], in1=whole[:, lo:hi, :].bitcast(I32), op=ALU.subtract)
+        def transpose_tables(first):
+            banks = [new_bank(), new_bank()]
+            for bank, part in zip(banks, (3, 1)):
+                for jj in range(QUAD):
+                    rows = rot_t[:, first + jj, part : part + 2, :].rearrange("p a i -> p (a i)")
+                    nc.tensor.transpose(bank[:, jj * P : (jj + 1) * P], rows, ident)
+            return banks
+
+        def channel_tables(first, banks):
+            cols = slice(first * P, first * P + BANK)
+            nc.scalar.copy(out=rot_c[:, 0, cols], in_=banks[0][:])
+            nc.scalar.activation(out=rot_c[:, 1, cols], in_=banks[1][:], func=ACT.Copy, scale=-1.0)
 
         w_grouped = {}
 
         def interleave_w(copy, group, g, lo, hi):
             if (group, g) not in w_grouped:
-                grouped = work.tile([P, BANK, 4], BF16, tag="w_grouped", name="w_grouped", align_bytes=64)
+                grouped = work.tile([P, BANK, 4], BF16, tag="w_grouped", name="w_grouped", bufs=3, align_bytes=64)
                 w_grouped[group, g] = grouped
             copy(
                 out=w_grouped[group, g][:, lo:hi, :].rearrange("p (c i) t -> p c t i", i=4),
@@ -163,11 +196,11 @@ def tile_baichuanattention_pa_kernel(tc, hidden, W_pack, conv_k, conv_v, out_0, 
 
         h_grouped = {}
 
-        def transpose_h(m, jj):
-            if m not in h_grouped:
+        def transpose_h(pair, jj):
+            if pair not in h_grouped:
                 grouped = work.tile([P, PASSES, 2, 4 * P], BF16, tag="h_grouped", name="h_grouped", bufs=3, align_bytes=64)
-                h_grouped[m] = grouped
-            words = h_raw[m][:, jj, :].bitcast(F32)
+                h_grouped[pair] = grouped
+            words = h_raw[pair][:, jj, :].bitcast(F32)
             bank = new_bank()
             for g in range(PASSES):
                 for u in range(2):
@@ -175,289 +208,233 @@ def tile_baichuanattention_pa_kernel(tc, hidden, W_pack, conv_k, conv_v, out_0, 
                     nc.tensor.transpose(bank[:, col : col + P], words[:, 256 * g + u : 256 * (g + 1) : 2], ident)
             return bank
 
-        def evacuate_h(copy, m, jj, bank):
-            copy(
-                out=h_grouped[m][:, :, jj, :].bitcast(F32).rearrange("p g (r u) -> p g r u", u=2),
+        def evacuate_h(pair, jj, bank):
+            nc.scalar.copy(
+                out=h_grouped[pair][:, :, jj, :].bitcast(F32).rearrange("p g (r u) -> p g r u", u=2),
                 in_=bank[:].rearrange("p (g u r) -> p g r u", g=PASSES, u=2),
             )
 
-        def quantize_h(m, lo, hi):
-            first = TILES - 2 - 2 * m
-            tok = slice((first + lo) * P, (first + hi) * P)
+        def quantize_h(pair, lo, hi):
+            tok = slice((2 * pair + lo) * P, (2 * pair + hi) * P)
             for g in range(PASSES):
                 nc.vector.quantize_mx(
                     out=h_codes[:, g, tok].bitcast(E5M2X4),
                     scales=h_scales[:, g, tok],
-                    in_=h_grouped[m][:, g, lo:hi, :].rearrange("p j c -> p (j c)"),
+                    in_=h_grouped[pair][:, g, lo:hi, :].rearrange("p j c -> p (j c)"),
                 )
 
-        def project_tokens(j, group):
-            bank = new_bank()
-            tok = slice(j * P, (j + 1) * P)
-            cols = slice(group * BANK, (group + 1) * BANK)
+        def project(out, h_cols, w_cols, tokens_on_partitions):
             for g in range(PASSES):
+                h_operand = (h_codes[:, g, h_cols].bitcast(E5M2X4), h_scales[:, g, h_cols])
+                w_operand = (w_codes[:, g, w_cols].bitcast(E4M3X4), w_scales[:, g, w_cols])
+                still, moving = (h_operand, w_operand) if tokens_on_partitions else (w_operand, h_operand)
                 nc.tensor.matmul_mx(
-                    out=bank[:],
-                    lhsT=h_codes[:, g, tok].bitcast(E5M2X4),
-                    lhsT_scale=h_scales[:, g, tok],
-                    rhs=w_codes[:, g, cols].bitcast(E4M3X4),
-                    rhs_scale=w_scales[:, g, cols],
+                    out=out,
+                    lhsT=still[0],
+                    lhsT_scale=still[1],
+                    rhs=moving[0],
+                    rhs_scale=moving[1],
                     start=(g == 0),
                     stop=(g == PASSES - 1),
                 )
-            return bank
 
-        def project_key_channels(quad, h):
+        def project_queries(tile, group):
             bank = new_bank()
-            tok = slice(quad * BANK, (quad + 1) * BANK)
-            cols = slice(KEYS * BANK + h * HEAD, KEYS * BANK + (h + 1) * HEAD)
-            for g in range(PASSES):
-                nc.tensor.matmul_mx(
-                    out=bank[:],
-                    lhsT=w_codes[:, g, cols].bitcast(E4M3X4),
-                    lhsT_scale=w_scales[:, g, cols],
-                    rhs=h_codes[:, g, tok].bitcast(E5M2X4),
-                    rhs_scale=h_scales[:, g, tok],
-                    start=(g == 0),
-                    stop=(g == PASSES - 1),
-                )
+            project(bank[:], slice(tile * P, (tile + 1) * P), slice(group * BANK, (group + 1) * BANK), True)
             return bank
 
-        def project_value_head(quad, h):
+        def project_keys(unit):
+            quad, h = divmod(unit, HEADS)
             bank = new_bank()
-            cols = slice(VALUES * BANK + h * HEAD, VALUES * BANK + (h + 1) * HEAD)
-            for jj in range(4):
-                tok = slice((4 * quad + jj) * P, (4 * quad + jj + 1) * P)
-                for g in range(PASSES):
-                    nc.tensor.matmul_mx(
-                        out=bank[:, jj * HEAD : (jj + 1) * HEAD],
-                        lhsT=h_codes[:, g, tok].bitcast(E5M2X4),
-                        lhsT_scale=h_scales[:, g, tok],
-                        rhs=w_codes[:, g, cols].bitcast(E4M3X4),
-                        rhs_scale=w_scales[:, g, cols],
-                        start=(g == 0),
-                        stop=(g == PASSES - 1),
-                    )
+            first = KEYS * BANK + h * HEAD
+            project(bank[:], slice(quad * BANK, (quad + 1) * BANK), slice(first, first + HEAD), False)
             return bank
 
-        def q_first(j, bank):
-            direct = work.tile([P, BANK], F32, tag="q_direct", name="q_direct", bufs=6)
-            crossed = work.tile([P, HEADS_PER_BANK, 2, HALF], F32, tag="q_crossed", name="q_crossed", bufs=3)
+        def project_values(unit):
+            quad, h = divmod(unit, HEADS)
+            bank = new_bank()
+            first = VALUES * BANK + h * HEAD
+            for jj in range(QUAD):
+                tile = QUAD * quad + jj
+                project(bank[:, jj * HEAD : (jj + 1) * HEAD], slice(tile * P, (tile + 1) * P), slice(first, first + HEAD), True)
+            return bank
+
+        q_terms = {}
+
+        def query_products(tile, group, bank):
+            pair, jj = divmod(tile, 2)
+            if jj == 0:
+                terms = work.tile([P, 2, HEADS, 2, HEAD], F32, tag="q_terms", name="q_terms")
+                q_terms[pair, group] = terms
+            slot = pair_place(pair)[1] + jj
             nc.vector.tensor_tensor(
-                out=direct[:].rearrange("p (a i) -> p a i", i=HALF),
-                in0=bank[:].rearrange("p (a i) -> p a i", i=HALF),
-                in1=cos_t[:, j, :].unsqueeze(1).to_broadcast([P, 8, HALF]),
+                out=q_terms[pair, group][:, jj, :, :, :].rearrange("p h r c -> p r h c"),
+                in0=bank[:].rearrange("p (h c) -> p h c", c=HEAD).unsqueeze(1).to_broadcast([P, 2, HEADS, HEAD]),
+                in1=rot_t[:, slot, 0:4, :].rearrange("p (r d) i -> p r (d i)", d=2).unsqueeze(2).to_broadcast([P, 2, HEADS, HEAD]),
                 op=ALU.mult,
             )
-            x = bank[:].rearrange("p (h d i) -> p h d i", d=2, i=HALF)
-            sin = sin_t[:, j, :].unsqueeze(1).to_broadcast([P, HEADS_PER_BANK, HALF])
-            nc.vector.tensor_tensor(out=crossed[:, :, 1, :], in0=x[:, :, 0, :], in1=sin, op=ALU.mult)
-            return direct, crossed
 
-        def q_second(j, group, bank, direct, crossed, adder):
-            x = bank[:].rearrange("p (h d i) -> p h d i", d=2, i=HALF)
-            sin = sin_t[:, j, :].unsqueeze(1).to_broadcast([P, HEADS_PER_BANK, HALF])
-            nc.vector.scalar_tensor_tensor(
-                out=crossed[:, :, 0, :], in0=x[:, :, 1, :], scalar=-1.0, in1=sin, op0=ALU.mult, op1=ALU.mult
+        def query_sums(pair, group, lo, hi, adder):
+            batch, first = pair_place(pair)
+            rotated = work.tile([P, hi - lo, BANK], F32, tag="q_rotated", name="q_rotated", bufs=3)
+            terms = q_terms[pair, group][:, lo:hi, :, :, :].rearrange("p j h r (d i) -> p (j h r) d i", d=2)
+            adder.tensor_tensor(
+                out=rotated[:].rearrange("p j (a i) -> p (j a) i", i=HALF), in0=terms[:, :, 0, :], in1=terms[:, :, 1, :], op=ALU.add
             )
-            adder.tensor_tensor(out=direct[:], in0=direct[:], in1=crossed[:].rearrange("p h d i -> p (h d i)"), op=ALU.add)
-            nc.sync.dma_start(out=q_out[:, j, group * BANK : (group + 1) * BANK], in_=direct[:])
+            nc.sync.dma_start(out=q_out[batch, :, first + lo : first + hi, group * BANK : (group + 1) * BANK], in_=rotated[:])
 
-        def rope_q(j, group, bank, adder):
-            direct, crossed = q_first(j, bank)
-            q_second(j, group, bank, direct, crossed, adder)
+        def key_products(unit, bank):
+            first = quad_place(unit // HEADS)[1]
+            terms = work.tile([P, 2, BANK], F32, tag="k_terms", name="k_terms", bufs=3)
+            nc.vector.tensor_tensor(
+                out=terms[:],
+                in0=bank[:].unsqueeze(1).to_broadcast([P, 2, BANK]),
+                in1=rot_c[:, :, first * P : first * P + BANK],
+                op=ALU.mult,
+            )
+            return terms
 
-        def rope_key_products(quad, bank):
-            parts = work.tile([P, 2, BANK], F32, tag="key_parts", name="key_parts", bufs=3)
-            x = bank[:].rearrange("p (j b t) -> p j b t", b=2, t=64)
-            for part, table in ((0, cos_c), (1, sin_c)):
-                nc.vector.tensor_tensor(
-                    out=parts[:, part, :].rearrange("p (j b t) -> p j b t", b=2, t=64),
-                    in0=x,
-                    in1=table[:, 4 * quad : 4 * quad + 4, :].unsqueeze(2).to_broadcast([P, 4, 2, 64]),
-                    op=ALU.mult,
-                )
-            return parts
-
-        def rope_key_sums(parts):
+        def key_sums(terms):
             bank = new_bank()
-            for jj in range(4):
+            for jj in range(QUAD):
                 tok = slice(jj * P, (jj + 1) * P)
-                nc.tensor.matmul(bank[:, tok], lhsT=parts[:, 0, tok], rhs=ident, is_transpose=True, start=True, stop=False)
-                nc.tensor.matmul(bank[:, tok], lhsT=parts[:, 1, tok], rhs=swap, is_transpose=True, start=False, stop=True)
+                nc.tensor.matmul(bank[:, tok], lhsT=terms[:, 0, tok], rhs=ident, is_transpose=True, start=True, stop=False)
+                nc.tensor.matmul(bank[:, tok], lhsT=terms[:, 1, tok], rhs=swap, is_transpose=True, start=False, stop=True)
             return bank
 
-        k_stage = keep.tile([P, TILES + 1, BANK], F32)
-        v_stage = keep.tile([P, TILES + 1, BANK], F32)
         taps_k16 = keep.tile([P, 8], BF16)
         taps_v16 = keep.tile([P, 8], BF16)
         taps_k = keep.tile([P, 8], F32)
         taps_v = keep.tile([P, 8], F32)
-        shift = keep.tile([P, P], F32)
+        inside = keep.tile([P, 1], F32)
+        carry_k = keep.tile([P, 8], F32)
+        carry_v = keep.tile([P, 8], F32)
 
-        def convolve(stage, taps, out, unit, bank, on_pool):
-            quad, h = 3 - unit // 4, unit % 4
+        def prepare_taps():
+            nc.gpsimd.tensor_scalar(out=inside[:], in0=position[:, 0:1], scalar1=float(SLOTS * (P - 1)), scalar2=None, op0=ALU.is_lt)
+            for raw, taps, carry in ((taps_k16, taps_k, carry_k), (taps_v16, taps_v, carry_v)):
+                nc.gpsimd.tensor_copy(out=taps[:], in_=raw[:])
+                nc.gpsimd.tensor_scalar(out=carry[:], in0=raw[:], scalar1=inside[:], scalar2=None, op0=ALU.mult)
+
+        def convolve(stage, last, taps, carry, out, unit, bank, on_pool):
+            quad, h = divmod(unit, HEADS)
+            batch, first = quad_place(quad)
+            upper = first > 0
             x = bank[:].rearrange("p (j c) -> p j c", c=HEAD)
             cols = slice(h * HEAD, (h + 1) * HEAD)
             w_prev, w_own = taps[:, 2 * h : 2 * h + 1], taps[:, 2 * h + 1 : 2 * h + 2]
-            lo = 1 if quad == 0 else 0
-            n = 3 if quad == 3 else 4
-            later = stage[:, 4 * quad + 1 : 4 * quad + 1 + n, cols]
-            nc.scalar.activation(out=stage[:, 4 * quad + lo : 4 * quad + 4, cols], in_=x[:, lo:4, :], func=ACT.Copy, scale=w_own)
-            if quad == 3:
-                nc.scalar.activation(out=stage[:, TILES, cols], in_=x[:, 3, :], func=ACT.Copy, scale=w_prev)
+            lo = 0 if upper else 1
+            n = QUAD - 1 if upper else QUAD
+            later = stage[:, batch, first + 1 : first + 1 + n, cols]
+            nc.scalar.activation(out=stage[:, batch, first + lo : first + QUAD, cols], in_=x[:, lo:QUAD, :], func=ACT.Copy, scale=w_own)
+            if upper:
+                nc.scalar.activation(out=last[:, batch, cols], in_=x[:, QUAD - 1, :], func=ACT.Copy, scale=carry[:, 2 * h : 2 * h + 1])
             if on_pool:
-                prev = work.tile([P, 5, HEAD], F32, tag="prev", name="prev", bufs=3)
-                nc.scalar.activation(out=prev[:, 1 : 1 + n, :], in_=x[:, 0:n, :], func=ACT.Copy, scale=w_prev)
-                if quad == 0:
-                    nc.scalar.activation(out=prev[:, 0, :], in_=x[:, 0, :], func=ACT.Copy, scale=w_own)
-                target = stage[:, 4 * quad + 1 - lo : 4 * quad + 1 + n, cols]
-                nc.gpsimd.tensor_tensor(out=target, in0=target, in1=prev[:, 1 - lo : 1 + n, :], op=ALU.add)
+                addend = work.tile([P, QUAD + 1, HEAD], F32, tag="addend", name="addend", bufs=3)
+                nc.scalar.activation(out=addend[:, 1 : 1 + n, :], in_=x[:, 0:n, :], func=ACT.Copy, scale=w_prev)
+                if not upper:
+                    nc.scalar.activation(out=addend[:, 0, :], in_=x[:, 0, :], func=ACT.Copy, scale=w_own)
+                target = stage[:, batch, first + 1 - lo : first + 1 + n, cols]
+                nc.gpsimd.tensor_tensor(out=target, in0=target, in1=addend[:, 1 - lo : 1 + n, :], op=ALU.add)
             else:
                 nc.vector.scalar_tensor_tensor(out=later, in0=x[:, 0:n, :], scalar=w_prev, in1=later, op0=ALU.mult, op1=ALU.add)
-                if quad == 0:
-                    first = stage[:, 0, cols]
-                    nc.vector.scalar_tensor_tensor(out=first, in0=x[:, 0, :], scalar=w_own, in1=first, op0=ALU.mult, op1=ALU.add)
-            if quad == 0:
-                nc.sync.dma_start(out=out[:, 0:5, cols], in_=stage[:, 0:5, cols])
-            elif h == HEADS_PER_BANK - 1:
-                nc.sync.dma_start(out=out[:, 4 * quad + 1 : 4 * quad + 1 + n, :], in_=stage[:, 4 * quad + 1 : 4 * quad + 1 + n, :])
+                if not upper:
+                    slot0 = stage[:, batch, 0, cols]
+                    nc.vector.scalar_tensor_tensor(out=slot0, in0=x[:, 0, :], scalar=w_own, in1=slot0, op0=ALU.mult, op1=ALU.add)
+            if upper and h == HEADS - 1:
+                for lo_row, hi_row in ((0, SHIFT_SPLIT), (SHIFT_SPLIT, P - 1)):
+                    nc.sync.dma_start(out=stage[lo_row + 1 : hi_row + 1, batch, 0, :], in_=last[lo_row:hi_row, batch, :])
+                nc.sync.dma_start(out=stage[0:1, batch, 0, :], in_=last[P - 1 : P, batch, :])
+                nc.sync.dma_start(out=out[batch, :, QUAD + 1 : SLOTS, :], in_=stage[:, batch, QUAD + 1 : SLOTS, :])
+            if not upper and h % 2 == 1:
+                both = slice((h - 1) * HEAD, (h + 1) * HEAD)
+                nc.sync.dma_start(out=out[batch, :, 0 : QUAD + 1, both], in_=stage[:, batch, 0 : QUAD + 1, both])
 
-        def shift_last_tile(stage):
-            wrap = new_bank()
-            nc.tensor.matmul(wrap[:], lhsT=shift[:], rhs=stage[:, TILES, :], start=True, stop=True)
-            nc.scalar.copy(out=stage[:, 0, :], in_=wrap[:])
-
-        FIRST = 14
-        turns_t(FIRST, TILES)
-        whole_t(FIRST, TILES)
-        frac_t(FIRST, TILES)
-        sin_cos(sin_t, cos_t, FIRST, TILES)
-        turns_t(0, FIRST)
-        interleave_w(nc.scalar.copy, Q0, 0, 0, BANK)
-        whole_t(0, FIRST)
-        evacuate_h(nc.scalar.copy, 0, 1, transpose_h(0, 1))
-        interleave_w(nc.vector.tensor_copy, Q0, 1, 0, BANK)
-        evacuate_h(nc.scalar.copy, 0, 0, transpose_h(0, 0))
+        nc.vector.tensor_tensor(out=turns, in0=turns, in1=whole, op=ALU.subtract)
+        interleave_w(nc.vector.tensor_copy, Q0, 0, 0, BANK)
+        token_tables(4, 6)
+        evacuate_h(0, 0, transpose_h(0, 0))
+        interleave_w(nc.scalar.copy, Q0, 1, 0, HEAD_SPLIT)
         quantize_w(Q0, 0)
-        quantize_h(0, 1, 2)
-        quantize_w(Q0, 1)
+        interleave_w(nc.vector.tensor_copy, Q0, 1, HEAD_SPLIT, BANK)
         quantize_h(0, 0, 1)
-        for jj in (1, 0):
-            evacuate_h(nc.scalar.copy, 1, jj, transpose_h(1, jj))
-        first_banks = [project_tokens(15, Q0), project_tokens(14, Q0)]
-        frac_t(0, FIRST)
-        sin_cos(sin_t, cos_t, 10, FIRST)
+        evacuate_h(0, 1, transpose_h(0, 1))
+        quantize_w(Q0, 1)
+        quantize_h(0, 1, 2)
+        for jj in range(2):
+            evacuate_h(1, jj, transpose_h(1, jj))
         quantize_h(1, 0, 2)
-        for jj in (1, 0):
-            evacuate_h(nc.scalar.copy, 2, jj, transpose_h(2, jj))
-        freq_col = keep.tile([P, 1], F32)
-        freq_bank = new_bank()
-        nc.tensor.transpose(freq_bank[:, 0:P], freq_row, ident)
-        nc.scalar.activation(out=freq_col[:], in_=freq_bank[:, 0:1], func=ACT.Copy, scale=sign[:])
-        sin_cos(sin_t, cos_t, 0, 10)
+        first_banks = [project_queries(tile, Q0) for tile in range(4)]
+        token_tables(6, 8)
+        interleave_w(nc.scalar.copy, KEYS, 0, 0, W_SPLIT)
+        for jj in range(2):
+            evacuate_h(2, jj, transpose_h(2, jj))
 
-        w_plan = {0: (KEYS, 0), 1: (KEYS, 1), 2: (VALUES, 0), 3: (VALUES, 1), 4: (Q1, 0), 5: (Q1, 1)}
+        w_plan = [(KEYS, 0), (KEYS, 1), (VALUES, 0), (VALUES, 1), (Q1, 0), (Q1, 1)]
         load_h(4, 0, 2)
         load_w(VALUES, 0)
         load_h(5, 0, 2)
         load_w(VALUES, 1)
-        load_h(6, 0, 2)
         nc.sync.dma_start(out=taps_v16[:], in_=conv_v.rearrange("h t -> (h t)").partition_broadcast(P))
         nc.sync.dma_start(out=taps_k16[:], in_=conv_k.rearrange("h t -> (h t)").partition_broadcast(P))
 
-        EARLY, K_FIRST, V_FIRST = 7, 3, 5
-        value_unit = 0
-        key_unit = 0
-        parts = None
-        for m in range(EARLY):
-            hi = TILES - 1 - 2 * m
-            with_k = m >= K_FIRST
-            with_v = m >= V_FIRST
-            if m == 0:
-                bank_hi, bank_lo = first_banks
-            else:
-                bank_hi = project_tokens(hi, Q0)
-            if with_k:
-                bank_k = project_key_channels(3 - key_unit // 4, key_unit % 4)
-            if m > 0:
-                bank_lo = project_tokens(hi - 1, Q0)
+        rounds = [[(2 * m, Q0), (2 * m + 1, Q0)] for m in range(PAIRS)] + [[(tile, Q1)] for tile in range(16)]
+        key_terms = None
+        for m, q_jobs in enumerate(rounds):
+            k_unit, v_unit = m - K_FIRST, m - V_FIRST
+            with_k = 0 <= k_unit < 16
+            with_v = 0 <= v_unit < 16
+            last_round = m == len(rounds) - 1
             if with_v:
-                bank_v = project_value_head(3 - value_unit // 4, value_unit % 4)
-            summed = parts
-            if summed is not None:
-                bank_kt = rope_key_sums(summed)
-            if m + 3 < 8:
-                h_banks = [transpose_h(m + 3, 1), transpose_h(m + 3, 0)]
-            rope_q(hi, Q0, bank_hi, nc.gpsimd)
-            if summed is not None:
-                convolve(k_stage, taps_k, k_out, key_unit - 1, bank_kt, True)
+                v_bank = project_values(v_unit)
+            q_banks = first_banks[2 * m : 2 * m + 2] if m < 2 else [project_queries(*job) for job in q_jobs]
             if with_k:
-                parts = rope_key_products(3 - key_unit // 4, bank_k)
-                key_unit += 1
-            direct, crossed = q_first(hi - 1, bank_lo)
+                k_bank = project_keys(k_unit)
+            if key_terms is not None:
+                summed = key_sums(key_terms)
+            if m + 3 < PAIRS:
+                h_banks = [transpose_h(m + 3, jj) for jj in range(2)]
+            if m in TABLES_AT:
+                table_banks = transpose_tables(TABLES_AT[m])
+
+            query_products(*q_jobs[0], q_banks[0])
             if with_v:
-                convolve(v_stage, taps_v, v_out, value_unit, bank_v, False)
-                value_unit += 1
-            if m < 3:
-                evacuate_h(nc.vector.tensor_copy, m + 3, 1, h_banks[0])
-            if m + 2 < 8:
-                quantize_h(m + 2, 0, 2)
-            if m - 1 in w_plan:
-                quantize_w(*w_plan[m - 1])
-            if m == 1 - 1:
-                nc.vector.tensor_scalar(out=whole_row.bitcast(I32), in0=pos_c_row, scalar1=freq_col[:], scalar2=None, op0=ALU.mult)
+                convolve(v_stage, v_last, taps_v, carry_v, v_out, v_unit, v_bank, v_unit in POOL_V)
+            if key_terms is not None:
+                convolve(k_stage, k_last, taps_k, carry_k, k_out, k_unit - 1, summed, True)
+            key_terms = key_products(k_unit, k_bank) if with_k else None
+            for job, bank in zip(q_jobs[1:], q_banks[1:]):
+                query_products(*job, bank)
             if m == 1:
-                nc.vector.scalar_tensor_tensor(
-                    out=frac_row, in0=pos_c_row, scalar=freq_col[:], in1=whole_row.bitcast(I32), op0=ALU.mult, op1=ALU.subtract
-                )
-            q_second(hi - 1, Q0, bank_lo, direct, crossed, nc.gpsimd)
-            if m + 3 < 8:
-                if m >= 3:
-                    evacuate_h(nc.scalar.copy, m + 3, 1, h_banks[0])
-                evacuate_h(nc.scalar.copy, m + 3, 0, h_banks[1])
-            if m == 2:
-                sin_cos(sin_c, cos_c, 0, TILES)
-            if m in w_plan:
-                interleave_w(nc.scalar.copy, w_plan[m][0], w_plan[m][1], 0, BANK)
+                quantize_h(2, 0, 2)
+            if 1 <= m < PAIRS - 2:
+                quantize_h(m + 2, 0, 2)
+            if m < len(w_plan) and W_SPLIT < BANK:
+                interleave_w(nc.vector.tensor_copy, *w_plan[m], W_SPLIT, BANK)
+            if 0 <= m - W_LAG < len(w_plan):
+                quantize_w(*w_plan[m - W_LAG])
+            tile, group = q_jobs[-1]
+            if last_round:
+                query_sums(tile // 2, group, 0, 1, nc.vector)
+                query_sums(tile // 2, group, 1, 2, nc.vector)
+            elif tile % 2 == 1:
+                query_sums(tile // 2, group, 0, 2, nc.gpsimd)
+            if m + 3 < PAIRS:
+                for jj in range(2):
+                    evacuate_h(m + 3, jj, h_banks[jj])
+            if m in TABLES_AT:
+                channel_tables(TABLES_AT[m], table_banks)
+            if m + 1 < len(w_plan):
+                interleave_w(nc.scalar.copy, *w_plan[m + 1], 0, W_SPLIT)
             if m == 0:
-                load_h(7, 0, 2)
+                load_h(6, 0, 2)
                 load_w(Q1, 0)
             if m == 1:
+                load_h(7, 0, 2)
                 load_w(Q1, 1)
-                nc.scalar.copy(out=taps_v[:], in_=taps_v16[:])
-                nc.scalar.copy(out=taps_k[:], in_=taps_k16[:])
-
-        if EARLY - 1 in w_plan:
-            quantize_w(*w_plan[EARLY - 1])
-
-        nc.gpsimd.memset(shift[:], 0.0)
-        nc.gpsimd.affine_select(
-            out=shift[:], in_=shift[:], compare_op=ALU.not_equal, fill=1.0, base=1, pattern=[[-1, P]], channel_multiplier=1
-        )
-        nc.gpsimd.memset(shift[:, 64:65], 0.0)
-        q_jobs = [(j, Q0) for j in range(TILES - 1 - 2 * EARLY, -1, -1)] + [(j, Q1) for j in range(TILES - 1, -1, -1)]
-        for step, (j, group) in enumerate(q_jobs):
-            with_k = key_unit < TILES
-            with_v = value_unit < TILES and True
-            bank_q = project_tokens(j, group)
-            if with_k:
-                bank_k = project_key_channels(3 - key_unit // 4, key_unit % 4)
-            if with_v:
-                bank_v = project_value_head(3 - value_unit // 4, value_unit % 4)
-            summed = parts
-            if summed is not None:
-                bank_kt = rope_key_sums(summed)
-            rope_q(j, group, bank_q, nc.gpsimd if step < len(q_jobs) - 0 else nc.vector)
-            parts = rope_key_products(3 - key_unit // 4, bank_k) if with_k else None
-            if with_v:
-                convolve(v_stage, taps_v, v_out, value_unit, bank_v, False)
-                value_unit += 1
-            if summed is not None:
-                convolve(k_stage, taps_k, k_out, key_unit - 1, bank_kt, True)
-            if with_k:
-                key_unit += 1
-            if step == 6:
-                shift_last_tile(v_stage)
-            if step == 2:
-                shift_last_tile(k_stage)
+            if m == LOWER_AT:
+                token_tables(0, 4)
+            if m + 2 in TABLES_AT:
+                second_cosine(TABLES_AT[m + 2])
+            if m == 2:
+                prepare_taps()

@@ -15,30 +15,31 @@ ACT = mybir.ActivationFunctionType
 
 P = 128
 K = 1024
-SLOTS = 8
-QUAD = 4
-QUADS = 4
-PAIRS = 8
 PASSES = 2
 K_PASS = 512
 BANK = 512
+BATCHES = 2
+SLOTS = 8
+QUAD = 4
+PAIRS = 8
+TILES = 16
+UNITS = 16
 HEAD = 128
 HALF = 64
 HEADS = 4
+TAPS = 2
 THETA = 100000.0
 Q0, Q1, KEYS, VALUES = 0, 1, 2, 3
+GROUPS = 4
 
-SHIFT_SPLIT = 112
+CARRY_SPLIT = 112
+
+KEYS_FROM = 3
+VALUES_FROM = 7
+LOWER_TABLES_AT = 2
+CHANNEL_TABLES_AT = {2: QUAD, 7: 0}
 
 FLOPS = 2 * 2048 * 1024 * 2048
-
-POOL_V = (0, 4)
-K_FIRST, V_FIRST = 3, 7
-TABLES_AT = {2: 4, 7: 0}
-W_SPLIT = 448
-HEAD_SPLIT = 128
-W_LAG = 1
-LOWER_AT = 2
 
 
 def tile_baichuanattention_pa_kernel(tc, hidden, W_pack, conv_k, conv_v, out_0, out_1, out_2):
@@ -49,7 +50,7 @@ def tile_baichuanattention_pa_kernel(tc, hidden, W_pack, conv_k, conv_v, out_0, 
     v_out = out_2.rearrange("b (p j) h d -> b p j (h d)", j=SLOTS)
 
     def quad_place(quad):
-        return quad % 2, QUAD * (1 - quad // 2)
+        return quad % BATCHES, QUAD * (1 - quad // BATCHES)
 
     def pair_place(pair):
         batch, first = quad_place(pair // 2)
@@ -61,14 +62,14 @@ def tile_baichuanattention_pa_kernel(tc, hidden, W_pack, conv_k, conv_v, out_0, 
         psum = ctx.enter_context(tc.psum_pool(name="psum", bufs=8))
         ctx.enter_context(tc.manual_schedule())
 
-        h_codes = keep.tile([P, PASSES, 16 * P], U32, align_bytes=64)
-        h_scales = keep.tile([P, PASSES, 16 * P], U8, align_bytes=64)
-        w_codes = keep.tile([P, PASSES, 4 * BANK], U32, align_bytes=64)
-        w_scales = keep.tile([P, PASSES, 4 * BANK], U8, align_bytes=64)
-        k_stage = keep.tile([P, 2, SLOTS, BANK], F32)
-        v_stage = keep.tile([P, 2, SLOTS, BANK], F32)
-        k_last = keep.tile([P, 2, BANK], F32)
-        v_last = keep.tile([P, 2, BANK], F32)
+        h_codes = keep.tile([P, PASSES, TILES * P], U32, align_bytes=64)
+        h_scales = keep.tile([P, PASSES, TILES * P], U8, align_bytes=64)
+        w_codes = keep.tile([P, PASSES, GROUPS * BANK], U32, align_bytes=64)
+        w_scales = keep.tile([P, PASSES, GROUPS * BANK], U8, align_bytes=64)
+        k_stage = keep.tile([P, BATCHES, SLOTS, BANK], F32)
+        v_stage = keep.tile([P, BATCHES, SLOTS, BANK], F32)
+        k_last = keep.tile([P, BATCHES, BANK], F32)
+        v_last = keep.tile([P, BATCHES, BANK], F32)
 
         def new_bank():
             bank = psum.tile([P, BANK], F32, tag="bank", name="bank")
@@ -143,6 +144,7 @@ def tile_baichuanattention_pa_kernel(tc, hidden, W_pack, conv_k, conv_v, out_0, 
             op=ALU.mult,
         )
         nc.vector.tensor_copy(out=whole, in_=turns)
+        nc.vector.tensor_tensor(out=turns, in0=turns, in1=whole, op=ALU.subtract)
 
         rot_t = keep.tile([P, SLOTS, 5, HALF], F32)
         rot_c = keep.tile([P, 2, SLOTS * P], F32)
@@ -159,7 +161,7 @@ def tile_baichuanattention_pa_kernel(tc, hidden, W_pack, conv_k, conv_v, out_0, 
                 bias=math.pi / 2,
             )
 
-        def second_cosine(first):
+        def repeat_cosine(first):
             nc.scalar.copy(out=rot_t[:, first : first + QUAD, 4, :], in_=rot_t[:, first : first + QUAD, 0, :])
 
         def transpose_tables(first):
@@ -175,15 +177,28 @@ def tile_baichuanattention_pa_kernel(tc, hidden, W_pack, conv_k, conv_v, out_0, 
             nc.scalar.copy(out=rot_c[:, 0, cols], in_=banks[0][:])
             nc.scalar.activation(out=rot_c[:, 1, cols], in_=banks[1][:], func=ACT.Copy, scale=-1.0)
 
+        taps_k16 = keep.tile([P, HEADS * TAPS], BF16)
+        taps_v16 = keep.tile([P, HEADS * TAPS], BF16)
+        taps_k = keep.tile([P, HEADS * TAPS], F32)
+        taps_v = keep.tile([P, HEADS * TAPS], F32)
+        inside = keep.tile([P, 1], F32)
+        carry_k = keep.tile([P, HEADS * TAPS], F32)
+        carry_v = keep.tile([P, HEADS * TAPS], F32)
+
+        def prepare_taps():
+            nc.gpsimd.tensor_scalar(out=inside[:], in0=position[:, 0:1], scalar1=float(SLOTS * (P - 1)), scalar2=None, op0=ALU.is_lt)
+            for raw, taps, carry in ((taps_k16, taps_k, carry_k), (taps_v16, taps_v, carry_v)):
+                nc.gpsimd.tensor_copy(out=taps[:], in_=raw[:])
+                nc.gpsimd.tensor_scalar(out=carry[:], in0=raw[:], scalar1=inside[:], scalar2=None, op0=ALU.mult)
+
         w_grouped = {}
 
-        def interleave_w(copy, group, g, lo, hi):
-            if (group, g) not in w_grouped:
-                grouped = work.tile([P, BANK, 4], BF16, tag="w_grouped", name="w_grouped", bufs=3, align_bytes=64)
-                w_grouped[group, g] = grouped
+        def interleave_w(copy, group, g):
+            grouped = work.tile([P, BANK, 4], BF16, tag="w_grouped", name="w_grouped", bufs=3, align_bytes=64)
+            w_grouped[group, g] = grouped
             copy(
-                out=w_grouped[group, g][:, lo:hi, :].rearrange("p (c i) t -> p c t i", i=4),
-                in_=w_raw[group, g][:, :, lo:hi].rearrange("p t (c i) -> p c t i", i=4),
+                out=grouped[:].rearrange("p (c i) t -> p c t i", i=4),
+                in_=w_raw[group, g][:].rearrange("p t (c i) -> p c t i", i=4),
             )
 
         def quantize_w(group, g):
@@ -259,6 +274,13 @@ def tile_baichuanattention_pa_kernel(tc, hidden, W_pack, conv_k, conv_v, out_0, 
                 project(bank[:, jj * HEAD : (jj + 1) * HEAD], slice(tile * P, (tile + 1) * P), slice(first, first + HEAD), True)
             return bank
 
+        waiting = []
+
+        def flush(count):
+            for out, in_ in waiting[:count]:
+                nc.sync.dma_start(out=out, in_=in_)
+            waiting[:count] = []
+
         q_terms = {}
 
         def query_products(tile, group, bank):
@@ -274,14 +296,20 @@ def tile_baichuanattention_pa_kernel(tc, hidden, W_pack, conv_k, conv_v, out_0, 
                 op=ALU.mult,
             )
 
-        def query_sums(pair, group, lo, hi, adder):
+        def query_sums(pair, group, lo, hi, adder, parts):
             batch, first = pair_place(pair)
             rotated = work.tile([P, hi - lo, BANK], F32, tag="q_rotated", name="q_rotated", bufs=3)
-            terms = q_terms[pair, group][:, lo:hi, :, :, :].rearrange("p j h r (d i) -> p (j h r) d i", d=2)
-            adder.tensor_tensor(
-                out=rotated[:].rearrange("p j (a i) -> p (j a) i", i=HALF), in0=terms[:, :, 0, :], in1=terms[:, :, 1, :], op=ALU.add
-            )
-            nc.sync.dma_start(out=q_out[batch, :, first + lo : first + hi, group * BANK : (group + 1) * BANK], in_=rotated[:])
+            for part in range(parts):
+                heads = slice(part * HEADS // parts, (part + 1) * HEADS // parts)
+                terms = q_terms[pair, group][:, lo:hi, heads, :, :].rearrange("p j h r (d i) -> p j (h r) d i", d=2)
+                sums = rotated[:].rearrange("p j (h c) -> p j h c", c=HEAD)[:, :, heads, :]
+                adder.tensor_tensor(
+                    out=sums.rearrange("p j h (r i) -> p j (h r) i", i=HALF),
+                    in0=terms[:, :, :, 0, :],
+                    in1=terms[:, :, :, 1, :],
+                    op=ALU.add,
+                )
+            waiting.append((q_out[batch, :, first + lo : first + hi, group * BANK : (group + 1) * BANK], rotated[:]))
 
         def key_products(unit, bank):
             first = quad_place(unit // HEADS)[1]
@@ -302,75 +330,74 @@ def tile_baichuanattention_pa_kernel(tc, hidden, W_pack, conv_k, conv_v, out_0, 
                 nc.tensor.matmul(bank[:, tok], lhsT=terms[:, 1, tok], rhs=swap, is_transpose=True, start=False, stop=True)
             return bank
 
-        taps_k16 = keep.tile([P, 8], BF16)
-        taps_v16 = keep.tile([P, 8], BF16)
-        taps_k = keep.tile([P, 8], F32)
-        taps_v = keep.tile([P, 8], F32)
-        inside = keep.tile([P, 1], F32)
-        carry_k = keep.tile([P, 8], F32)
-        carry_v = keep.tile([P, 8], F32)
-
-        def prepare_taps():
-            nc.gpsimd.tensor_scalar(out=inside[:], in0=position[:, 0:1], scalar1=float(SLOTS * (P - 1)), scalar2=None, op0=ALU.is_lt)
-            for raw, taps, carry in ((taps_k16, taps_k, carry_k), (taps_v16, taps_v, carry_v)):
-                nc.gpsimd.tensor_copy(out=taps[:], in_=raw[:])
-                nc.gpsimd.tensor_scalar(out=carry[:], in0=raw[:], scalar1=inside[:], scalar2=None, op0=ALU.mult)
-
-        def convolve(stage, last, taps, carry, out, unit, bank, on_pool):
+        def convolve(stage, last, taps, carry, out, unit, bank, on_gpsimd):
             quad, h = divmod(unit, HEADS)
             batch, first = quad_place(quad)
             upper = first > 0
             x = bank[:].rearrange("p (j c) -> p j c", c=HEAD)
             cols = slice(h * HEAD, (h + 1) * HEAD)
-            w_prev, w_own = taps[:, 2 * h : 2 * h + 1], taps[:, 2 * h + 1 : 2 * h + 2]
-            lo = 0 if upper else 1
+            w_prev, w_own = taps[:, TAPS * h : TAPS * h + 1], taps[:, TAPS * h + 1 : TAPS * h + 2]
+            written_from = 0 if upper else 1
             n = QUAD - 1 if upper else QUAD
-            later = stage[:, batch, first + 1 : first + 1 + n, cols]
-            nc.scalar.activation(out=stage[:, batch, first + lo : first + QUAD, cols], in_=x[:, lo:QUAD, :], func=ACT.Copy, scale=w_own)
+            nc.scalar.activation(
+                out=stage[:, batch, first + written_from : first + QUAD, cols], in_=x[:, written_from:QUAD, :], func=ACT.Copy, scale=w_own
+            )
             if upper:
-                nc.scalar.activation(out=last[:, batch, cols], in_=x[:, QUAD - 1, :], func=ACT.Copy, scale=carry[:, 2 * h : 2 * h + 1])
-            if on_pool:
+                nc.scalar.activation(
+                    out=last[:, batch, cols], in_=x[:, QUAD - 1, :], func=ACT.Copy, scale=carry[:, TAPS * h : TAPS * h + 1]
+                )
+            if on_gpsimd:
                 addend = work.tile([P, QUAD + 1, HEAD], F32, tag="addend", name="addend", bufs=3)
                 nc.scalar.activation(out=addend[:, 1 : 1 + n, :], in_=x[:, 0:n, :], func=ACT.Copy, scale=w_prev)
                 if not upper:
                     nc.scalar.activation(out=addend[:, 0, :], in_=x[:, 0, :], func=ACT.Copy, scale=w_own)
-                target = stage[:, batch, first + 1 - lo : first + 1 + n, cols]
-                nc.gpsimd.tensor_tensor(out=target, in0=target, in1=addend[:, 1 - lo : 1 + n, :], op=ALU.add)
+                target = stage[:, batch, first + 1 - written_from : first + 1 + n, cols]
+                nc.gpsimd.tensor_tensor(out=target, in0=target, in1=addend[:, 1 - written_from : 1 + n, :], op=ALU.add)
             else:
+                later = stage[:, batch, first + 1 : first + 1 + n, cols]
                 nc.vector.scalar_tensor_tensor(out=later, in0=x[:, 0:n, :], scalar=w_prev, in1=later, op0=ALU.mult, op1=ALU.add)
                 if not upper:
                     slot0 = stage[:, batch, 0, cols]
                     nc.vector.scalar_tensor_tensor(out=slot0, in0=x[:, 0, :], scalar=w_own, in1=slot0, op0=ALU.mult, op1=ALU.add)
+
+            finished = None
             if upper and h == HEADS - 1:
-                for lo_row, hi_row in ((0, SHIFT_SPLIT), (SHIFT_SPLIT, P - 1)):
+                for lo_row, hi_row in ((0, CARRY_SPLIT), (CARRY_SPLIT, P - 1)):
                     nc.sync.dma_start(out=stage[lo_row + 1 : hi_row + 1, batch, 0, :], in_=last[lo_row:hi_row, batch, :])
                 nc.sync.dma_start(out=stage[0:1, batch, 0, :], in_=last[P - 1 : P, batch, :])
-                nc.sync.dma_start(out=out[batch, :, QUAD + 1 : SLOTS, :], in_=stage[:, batch, QUAD + 1 : SLOTS, :])
-            if not upper and h % 2 == 1:
-                both = slice((h - 1) * HEAD, (h + 1) * HEAD)
-                nc.sync.dma_start(out=out[batch, :, 0 : QUAD + 1, both], in_=stage[:, batch, 0 : QUAD + 1, both])
+                finished = (slice(QUAD + 1, SLOTS), slice(0, BANK))
+            elif unit >= UNITS - 2:
+                finished = (slice(0, QUAD + 1), cols)
+            elif not upper and h % 2 == 1:
+                finished = (slice(0, QUAD + 1), slice((h - 1) * HEAD, (h + 1) * HEAD))
+            if finished is not None:
+                store = (out[batch, :, finished[0], finished[1]], stage[:, batch, finished[0], finished[1]])
+                if on_gpsimd:
+                    waiting.append(store)
+                else:
+                    nc.sync.dma_start(out=store[0], in_=store[1])
 
-        nc.vector.tensor_tensor(out=turns, in0=turns, in1=whole, op=ALU.subtract)
-        interleave_w(nc.vector.tensor_copy, Q0, 0, 0, BANK)
-        token_tables(4, 6)
+        interleave_w(nc.vector.tensor_copy, Q0, 0)
+        token_tables(QUAD, QUAD + 2)
         evacuate_h(0, 0, transpose_h(0, 0))
-        interleave_w(nc.scalar.copy, Q0, 1, 0, HEAD_SPLIT)
+        interleave_w(nc.vector.tensor_copy, Q0, 1)
         quantize_w(Q0, 0)
-        interleave_w(nc.vector.tensor_copy, Q0, 1, HEAD_SPLIT, BANK)
         quantize_h(0, 0, 1)
         evacuate_h(0, 1, transpose_h(0, 1))
         quantize_w(Q0, 1)
         quantize_h(0, 1, 2)
         for jj in range(2):
             evacuate_h(1, jj, transpose_h(1, jj))
+        first_banks = [project_queries(tile, Q0) for tile in range(2)]
+        query_products(0, Q0, first_banks[0])
         quantize_h(1, 0, 2)
-        first_banks = [project_queries(tile, Q0) for tile in range(4)]
-        token_tables(6, 8)
-        interleave_w(nc.scalar.copy, KEYS, 0, 0, W_SPLIT)
+        third_pair = [transpose_h(2, jj) for jj in range(2)]
+        first_banks += [project_queries(tile, Q0) for tile in range(2, 4)]
+        token_tables(QUAD + 2, SLOTS)
+        interleave_w(nc.scalar.copy, KEYS, 0)
         for jj in range(2):
-            evacuate_h(2, jj, transpose_h(2, jj))
+            evacuate_h(2, jj, third_pair[jj])
 
-        w_plan = [(KEYS, 0), (KEYS, 1), (VALUES, 0), (VALUES, 1), (Q1, 0), (Q1, 1)]
         load_h(4, 0, 2)
         load_w(VALUES, 0)
         load_h(5, 0, 2)
@@ -378,63 +405,68 @@ def tile_baichuanattention_pa_kernel(tc, hidden, W_pack, conv_k, conv_v, out_0, 
         nc.sync.dma_start(out=taps_v16[:], in_=conv_v.rearrange("h t -> (h t)").partition_broadcast(P))
         nc.sync.dma_start(out=taps_k16[:], in_=conv_k.rearrange("h t -> (h t)").partition_broadcast(P))
 
-        rounds = [[(2 * m, Q0), (2 * m + 1, Q0)] for m in range(PAIRS)] + [[(tile, Q1)] for tile in range(16)]
-        key_terms = None
+        rounds = [[(2 * pair, Q0), (2 * pair + 1, Q0)] for pair in range(PAIRS)] + [[(tile, Q1)] for tile in range(TILES)]
+        w_chunks = [(KEYS, 0), (KEYS, 1), (VALUES, 0), (VALUES, 1), (Q1, 0), (Q1, 1)]
+        interleave_at = {0: 1, 2: 2, 3: 3, 4: 4, 5: 5}
+        quantize_at = {1: [2, 3], 2: [4], 3: [5], 4: [6], 5: [7]}
+        convolve_keys_at = {KEYS_FROM + unit + (1 if unit < UNITS - 1 else 2): unit for unit in range(UNITS)}
+        key_terms = {}
         for m, q_jobs in enumerate(rounds):
-            k_unit, v_unit = m - K_FIRST, m - V_FIRST
-            with_k = 0 <= k_unit < 16
-            with_v = 0 <= v_unit < 16
-            last_round = m == len(rounds) - 1
+            k_unit, v_unit = m - KEYS_FROM, m - VALUES_FROM
+            with_k = 0 <= k_unit < UNITS
+            with_v = 0 <= v_unit < UNITS
+            from_earlier_rounds = len(waiting)
+
             if with_v:
                 v_bank = project_values(v_unit)
             q_banks = first_banks[2 * m : 2 * m + 2] if m < 2 else [project_queries(*job) for job in q_jobs]
             if with_k:
                 k_bank = project_keys(k_unit)
-            if key_terms is not None:
-                summed = key_sums(key_terms)
+            if m in convolve_keys_at:
+                summed = key_sums(key_terms[convolve_keys_at[m]])
             if m + 3 < PAIRS:
                 h_banks = [transpose_h(m + 3, jj) for jj in range(2)]
-            if m in TABLES_AT:
-                table_banks = transpose_tables(TABLES_AT[m])
+            if m in CHANNEL_TABLES_AT:
+                table_banks = transpose_tables(CHANNEL_TABLES_AT[m])
 
-            query_products(*q_jobs[0], q_banks[0])
+            if m > 0:
+                query_products(*q_jobs[0], q_banks[0])
             if with_v:
-                convolve(v_stage, v_last, taps_v, carry_v, v_out, v_unit, v_bank, v_unit in POOL_V)
-            if key_terms is not None:
-                convolve(k_stage, k_last, taps_k, carry_k, k_out, k_unit - 1, summed, True)
-            key_terms = key_products(k_unit, k_bank) if with_k else None
+                on_gpsimd = v_unit % HEADS == 0 and v_unit < UNITS // 2
+                convolve(v_stage, v_last, taps_v, carry_v, v_out, v_unit, v_bank, on_gpsimd)
+            if m in convolve_keys_at:
+                convolve(k_stage, k_last, taps_k, carry_k, k_out, convolve_keys_at[m], summed, True)
+            if with_k:
+                key_terms[k_unit] = key_products(k_unit, k_bank)
             for job, bank in zip(q_jobs[1:], q_banks[1:]):
                 query_products(*job, bank)
-            if m == 1:
-                quantize_h(2, 0, 2)
-            if 1 <= m < PAIRS - 2:
-                quantize_h(m + 2, 0, 2)
-            if m < len(w_plan) and W_SPLIT < BANK:
-                interleave_w(nc.vector.tensor_copy, *w_plan[m], W_SPLIT, BANK)
-            if 0 <= m - W_LAG < len(w_plan):
-                quantize_w(*w_plan[m - W_LAG])
+
+            for pair in quantize_at.get(m, []):
+                quantize_h(pair, 0, 2)
+            if 1 <= m <= len(w_chunks):
+                quantize_w(*w_chunks[m - 1])
             tile, group = q_jobs[-1]
-            if last_round:
-                query_sums(tile // 2, group, 0, 1, nc.vector)
-                query_sums(tile // 2, group, 1, 2, nc.vector)
+            if m == len(rounds) - 1:
+                query_sums(tile // 2, group, 0, 1, nc.vector, 1)
+                query_sums(tile // 2, group, 1, 2, nc.vector, 1)
             elif tile % 2 == 1:
-                query_sums(tile // 2, group, 0, 2, nc.gpsimd)
+                query_sums(tile // 2, group, 0, 2, nc.gpsimd, 2 if m <= len(w_chunks) else 1)
+            flush(from_earlier_rounds if m >= PAIRS else len(waiting))
+
             if m + 3 < PAIRS:
                 for jj in range(2):
                     evacuate_h(m + 3, jj, h_banks[jj])
-            if m in TABLES_AT:
-                channel_tables(TABLES_AT[m], table_banks)
-            if m + 1 < len(w_plan):
-                interleave_w(nc.scalar.copy, *w_plan[m + 1], 0, W_SPLIT)
-            if m == 0:
-                load_h(6, 0, 2)
-                load_w(Q1, 0)
-            if m == 1:
-                load_h(7, 0, 2)
-                load_w(Q1, 1)
-            if m == LOWER_AT:
-                token_tables(0, 4)
-            if m + 2 in TABLES_AT:
-                second_cosine(TABLES_AT[m + 2])
-            if m == 2:
+            if m in CHANNEL_TABLES_AT:
+                channel_tables(CHANNEL_TABLES_AT[m], table_banks)
+            if m in interleave_at:
+                interleave_w(nc.scalar.copy, *w_chunks[interleave_at[m]])
+            if m < PASSES:
+                load_h(PAIRS - 2 + m, 0, 2)
+                load_w(Q1, m)
+            if m == LOWER_TABLES_AT:
+                token_tables(0, QUAD)
+            if m + 2 in CHANNEL_TABLES_AT:
+                repeat_cosine(CHANNEL_TABLES_AT[m + 2])
+            if m == KEYS_FROM - 1:
                 prepare_taps()
+        flush(len(waiting))

import math
from contextlib import ExitStack

import concourse.mybir as mybir

F32 = mybir.dt.float32
BF16 = mybir.dt.bfloat16
I32 = mybir.dt.int32
U32 = mybir.dt.uint32
U8 = mybir.dt.uint8
E5M2X4 = mybir.dt.float8_e5m2_x4
E4M3X4 = mybir.dt.float8_e4m3fn_x4
ALU = mybir.AluOpType
ACT = mybir.ActivationFunctionType

P = 128
K = 1024
PASSES = 2
K_PASS = 512
BANK = 512
BATCHES = 2
SLOTS = 8
QUAD = 4
PAIRS = 8
TILES = 16
UNITS = 16
HEAD = 128
HALF = 64
HEADS = 4
TAPS = 2
THETA = 100000.0
Q0, Q1, KEYS, VALUES = 0, 1, 2, 3
GROUPS = 4

CARRY_SPLIT = 112

KEYS_FROM = 3
VALUES_FROM = 7
LOWER_TABLES_AT = 2
CHANNEL_TABLES_AT = {2: QUAD, 7: 0}

FLOPS = 2 * 2048 * 1024 * 2048


def tile_baichuanattention_pa_kernel(tc, hidden, W_pack, conv_k, conv_v, out_0, out_1, out_2):
    nc = tc.nc
    hid = hidden.rearrange("b (p j) k -> b p j k", j=SLOTS)
    q_out = out_0.rearrange("b (p j) h d -> b p j (h d)", j=SLOTS)
    k_out = out_1.rearrange("b (p j) h d -> b p j (h d)", j=SLOTS)
    v_out = out_2.rearrange("b (p j) h d -> b p j (h d)", j=SLOTS)

    def quad_place(quad):
        return quad % BATCHES, QUAD * (1 - quad // BATCHES)

    def pair_place(pair):
        batch, first = quad_place(pair // 2)
        return batch, first + 2 * (pair % 2)

    with ExitStack() as ctx:
        keep = ctx.enter_context(tc.tile_pool(name="keep", bufs=1))
        work = ctx.enter_context(tc.tile_pool(name="work", bufs=2))
        psum = ctx.enter_context(tc.psum_pool(name="psum", bufs=8))
        ctx.enter_context(tc.manual_schedule())

        h_codes = keep.tile([P, PASSES, TILES * P], U32, align_bytes=64)
        h_scales = keep.tile([P, PASSES, TILES * P], U8, align_bytes=64)
        w_codes = keep.tile([P, PASSES, GROUPS * BANK], U32, align_bytes=64)
        w_scales = keep.tile([P, PASSES, GROUPS * BANK], U8, align_bytes=64)
        k_stage = keep.tile([P, BATCHES, SLOTS, BANK], F32)
        v_stage = keep.tile([P, BATCHES, SLOTS, BANK], F32)
        k_last = keep.tile([P, BATCHES, BANK], F32)
        v_last = keep.tile([P, BATCHES, BANK], F32)

        def new_bank():
            bank = psum.tile([P, BANK], F32, tag="bank", name="bank")
            return bank

        w_raw = {}
        h_raw = {}

        def load_w(group, g):
            raw = work.tile([P, 4, BANK], BF16, tag="w_raw", name="w_raw", bufs=4)
            rows = W_pack[g * K_PASS : (g + 1) * K_PASS, group * BANK : (group + 1) * BANK]
            nc.sync.dma_start(out=raw[:], in_=rows.rearrange("(p t) n -> p t n", t=4))
            w_raw[group, g] = raw

        def load_h(pair, lo, hi):
            if pair not in h_raw:
                raw = work.tile([P, 2, K], BF16, tag="h_raw", name="h_raw", bufs=4)
                h_raw[pair] = raw
            batch, first = pair_place(pair)
            nc.sync.dma_start(out=h_raw[pair][:, lo:hi, :], in_=hid[batch, :, first + lo : first + hi, :])

        load_w(Q0, 0)
        load_h(0, 0, 1)
        load_w(Q0, 1)
        load_h(0, 1, 2)
        load_h(1, 0, 2)
        load_h(2, 0, 2)
        load_w(KEYS, 0)
        load_h(3, 0, 2)
        load_w(KEYS, 1)

        eye2 = keep.tile([P, 2, P], F32)
        eye_row = eye2[:].rearrange("p d n -> p (d n)")
        ident = eye_row[:, 0:P]
        swap = eye_row[:, HALF : HALF + P]
        position = keep.tile([P, SLOTS], F32)
        nc.gpsimd.iota(position[:], [[1, SLOTS]], base=0, channel_multiplier=SLOTS, allow_small_or_imprecise_dtypes=True)
        nc.gpsimd.memset(eye_row, 0.0)
        nc.gpsimd.affine_select(
            out=eye2[:],
            in_=eye2[:],
            compare_op=ALU.not_equal,
            fill=1.0,
            base=0,
            pattern=[[0, 2], [-1, P]],
            channel_multiplier=1,
        )

        ones = keep.tile([P, 1], F32)
        nc.vector.memset(ones[:], 1.0)
        coarse = keep.tile([P, 8], F32)
        fine = keep.tile([P, 8], F32)
        for a in range(8):
            nc.vector.tensor_scalar(
                out=coarse[:, a : a + 1], in0=ones[:], scalar1=THETA ** (-8 * a / HALF) / (2 * math.pi), scalar2=None, op0=ALU.mult
            )
            nc.vector.tensor_scalar(out=fine[:, a : a + 1], in0=ones[:], scalar1=THETA ** (-a / HALF), scalar2=None, op0=ALU.mult)
        freq = keep.tile([P, 8, 8], F32)
        nc.vector.tensor_tensor(
            out=freq[:],
            in0=coarse[:].unsqueeze(2).to_broadcast([P, 8, 8]),
            in1=fine[:].unsqueeze(1).to_broadcast([P, 8, 8]),
            op=ALU.mult,
        )
        turns = v_stage[:, 1, 1, :].rearrange("p (j i) -> p j i", i=HALF)
        whole = v_stage[:, 1, 2, :].bitcast(I32).rearrange("p (j i) -> p j i", i=HALF)
        size = v_stage[:, 1, 3, :].rearrange("p (j i) -> p j i", i=HALF)
        nc.vector.tensor_tensor(
            out=turns,
            in0=position[:].unsqueeze(2).to_broadcast([P, SLOTS, HALF]),
            in1=freq[:].rearrange("p a b -> p (a b)").unsqueeze(1).to_broadcast([P, SLOTS, HALF]),
            op=ALU.mult,
        )
        nc.vector.tensor_copy(out=whole, in_=turns)
        nc.vector.tensor_tensor(out=turns, in0=turns, in1=whole, op=ALU.subtract)

        rot_t = keep.tile([P, SLOTS, 5, HALF], F32)
        rot_c = keep.tile([P, 2, SLOTS * P], F32)

        def token_tables(lo, hi):
            nc.scalar.activation(out=rot_t[:, lo:hi, 1, :], in_=turns[:, lo:hi, :], func=ACT.Sin, scale=-2 * math.pi)
            nc.scalar.activation(out=size[:, lo:hi, :], in_=turns[:, lo:hi, :], func=ACT.Abs)
            nc.scalar.activation(out=rot_t[:, lo:hi, 2, :], in_=turns[:, lo:hi, :], func=ACT.Sin, scale=2 * math.pi)
            nc.scalar.activation(
                out=rot_t[:, lo:hi, 0:4:3, :],
                in_=size[:, lo:hi, :].unsqueeze(2).to_broadcast([P, hi - lo, 2, HALF]),
                func=ACT.Sin,
                scale=-2 * math.pi,
                bias=math.pi / 2,
            )

        def repeat_cosine(first):
            nc.scalar.copy(out=rot_t[:, first : first + QUAD, 4, :], in_=rot_t[:, first : first + QUAD, 0, :])

        def transpose_tables(first):
            banks = [new_bank(), new_bank()]
            for bank, part in zip(banks, (3, 1)):
                for jj in range(QUAD):
                    rows = rot_t[:, first + jj, part : part + 2, :].rearrange("p a i -> p (a i)")
                    nc.tensor.transpose(bank[:, jj * P : (jj + 1) * P], rows, ident)
            return banks

        def channel_tables(first, banks):
            cols = slice(first * P, first * P + BANK)
            nc.scalar.copy(out=rot_c[:, 0, cols], in_=banks[0][:])
            nc.scalar.activation(out=rot_c[:, 1, cols], in_=banks[1][:], func=ACT.Copy, scale=-1.0)

        taps_k16 = keep.tile([P, HEADS * TAPS], BF16)
        taps_v16 = keep.tile([P, HEADS * TAPS], BF16)
        taps_k = keep.tile([P, HEADS * TAPS], F32)
        taps_v = keep.tile([P, HEADS * TAPS], F32)
        inside = keep.tile([P, 1], F32)
        carry_k = keep.tile([P, HEADS * TAPS], F32)
        carry_v = keep.tile([P, HEADS * TAPS], F32)

        def prepare_taps():
            nc.gpsimd.tensor_scalar(out=inside[:], in0=position[:, 0:1], scalar1=float(SLOTS * (P - 1)), scalar2=None, op0=ALU.is_lt)
            for raw, taps, carry in ((taps_k16, taps_k, carry_k), (taps_v16, taps_v, carry_v)):
                nc.gpsimd.tensor_copy(out=taps[:], in_=raw[:])
                nc.gpsimd.tensor_scalar(out=carry[:], in0=raw[:], scalar1=inside[:], scalar2=None, op0=ALU.mult)

        w_grouped = {}

        def interleave_w(copy, group, g):
            grouped = work.tile([P, BANK, 4], BF16, tag="w_grouped", name="w_grouped", bufs=3, align_bytes=64)
            w_grouped[group, g] = grouped
            copy(
                out=grouped[:].rearrange("p (c i) t -> p c t i", i=4),
                in_=w_raw[group, g][:].rearrange("p t (c i) -> p c t i", i=4),
            )

        def quantize_w(group, g):
            cols = slice(group * BANK, (group + 1) * BANK)
            nc.vector.quantize_mx(
                out=w_codes[:, g, cols].bitcast(E4M3X4),
                scales=w_scales[:, g, cols],
                in_=w_grouped[group, g][:].rearrange("p n t -> p (n t)"),
            )

        h_grouped = {}

        def transpose_h(pair, jj):
            if pair not in h_grouped:
                grouped = work.tile([P, PASSES, 2, 4 * P], BF16, tag="h_grouped", name="h_grouped", bufs=3, align_bytes=64)
                h_grouped[pair] = grouped
            words = h_raw[pair][:, jj, :].bitcast(F32)
            bank = new_bank()
            for g in range(PASSES):
                for u in range(2):
                    col = (2 * g + u) * P
                    nc.tensor.transpose(bank[:, col : col + P], words[:, 256 * g + u : 256 * (g + 1) : 2], ident)
            return bank

        def evacuate_h(pair, jj, bank):
            nc.scalar.copy(
                out=h_grouped[pair][:, :, jj, :].bitcast(F32).rearrange("p g (r u) -> p g r u", u=2),
                in_=bank[:].rearrange("p (g u r) -> p g r u", g=PASSES, u=2),
            )

        def quantize_h(pair, lo, hi):
            tok = slice((2 * pair + lo) * P, (2 * pair + hi) * P)
            for g in range(PASSES):
                nc.vector.quantize_mx(
                    out=h_codes[:, g, tok].bitcast(E5M2X4),
                    scales=h_scales[:, g, tok],
                    in_=h_grouped[pair][:, g, lo:hi, :].rearrange("p j c -> p (j c)"),
                )

        def project(out, h_cols, w_cols, tokens_on_partitions):
            for g in range(PASSES):
                h_operand = (h_codes[:, g, h_cols].bitcast(E5M2X4), h_scales[:, g, h_cols])
                w_operand = (w_codes[:, g, w_cols].bitcast(E4M3X4), w_scales[:, g, w_cols])
                still, moving = (h_operand, w_operand) if tokens_on_partitions else (w_operand, h_operand)
                nc.tensor.matmul_mx(
                    out=out,
                    lhsT=still[0],
                    lhsT_scale=still[1],
                    rhs=moving[0],
                    rhs_scale=moving[1],
                    start=(g == 0),
                    stop=(g == PASSES - 1),
                )

        def project_queries(tile, group):
            bank = new_bank()
            project(bank[:], slice(tile * P, (tile + 1) * P), slice(group * BANK, (group + 1) * BANK), True)
            return bank

        def project_keys(unit):
            quad, h = divmod(unit, HEADS)
            bank = new_bank()
            first = KEYS * BANK + h * HEAD
            project(bank[:], slice(quad * BANK, (quad + 1) * BANK), slice(first, first + HEAD), False)
            return bank

        def project_values(unit):
            quad, h = divmod(unit, HEADS)
            bank = new_bank()
            first = VALUES * BANK + h * HEAD
            for jj in range(QUAD):
                tile = QUAD * quad + jj
                project(bank[:, jj * HEAD : (jj + 1) * HEAD], slice(tile * P, (tile + 1) * P), slice(first, first + HEAD), True)
            return bank

        waiting = []

        def flush(count):
            for out, in_ in waiting[:count]:
                nc.sync.dma_start(out=out, in_=in_)
            waiting[:count] = []

        q_terms = {}

        def query_products(tile, group, bank):
            pair, jj = divmod(tile, 2)
            if jj == 0:
                terms = work.tile([P, 2, HEADS, 2, HEAD], F32, tag="q_terms", name="q_terms")
                q_terms[pair, group] = terms
            slot = pair_place(pair)[1] + jj
            nc.vector.tensor_tensor(
                out=q_terms[pair, group][:, jj, :, :, :].rearrange("p h r c -> p r h c"),
                in0=bank[:].rearrange("p (h c) -> p h c", c=HEAD).unsqueeze(1).to_broadcast([P, 2, HEADS, HEAD]),
                in1=rot_t[:, slot, 0:4, :].rearrange("p (r d) i -> p r (d i)", d=2).unsqueeze(2).to_broadcast([P, 2, HEADS, HEAD]),
                op=ALU.mult,
            )

        def query_sums(pair, group, lo, hi, adder, parts):
            batch, first = pair_place(pair)
            rotated = work.tile([P, hi - lo, BANK], F32, tag="q_rotated", name="q_rotated", bufs=3)
            for part in range(parts):
                heads = slice(part * HEADS // parts, (part + 1) * HEADS // parts)
                terms = q_terms[pair, group][:, lo:hi, heads, :, :].rearrange("p j h r (d i) -> p j (h r) d i", d=2)
                sums = rotated[:].rearrange("p j (h c) -> p j h c", c=HEAD)[:, :, heads, :]
                adder.tensor_tensor(
                    out=sums.rearrange("p j h (r i) -> p j (h r) i", i=HALF),
                    in0=terms[:, :, :, 0, :],
                    in1=terms[:, :, :, 1, :],
                    op=ALU.add,
                )
            waiting.append((q_out[batch, :, first + lo : first + hi, group * BANK : (group + 1) * BANK], rotated[:]))

        def key_products(unit, bank):
            first = quad_place(unit // HEADS)[1]
            terms = work.tile([P, 2, BANK], F32, tag="k_terms", name="k_terms", bufs=3)
            nc.vector.tensor_tensor(
                out=terms[:],
                in0=bank[:].unsqueeze(1).to_broadcast([P, 2, BANK]),
                in1=rot_c[:, :, first * P : first * P + BANK],
                op=ALU.mult,
            )
            return terms

        def key_sums(terms):
            bank = new_bank()
            for jj in range(QUAD):
                tok = slice(jj * P, (jj + 1) * P)
                nc.tensor.matmul(bank[:, tok], lhsT=terms[:, 0, tok], rhs=ident, is_transpose=True, start=True, stop=False)
                nc.tensor.matmul(bank[:, tok], lhsT=terms[:, 1, tok], rhs=swap, is_transpose=True, start=False, stop=True)
            return bank

        def convolve(stage, last, taps, carry, out, unit, bank, on_gpsimd):
            quad, h = divmod(unit, HEADS)
            batch, first = quad_place(quad)
            upper = first > 0
            x = bank[:].rearrange("p (j c) -> p j c", c=HEAD)
            cols = slice(h * HEAD, (h + 1) * HEAD)
            w_prev, w_own = taps[:, TAPS * h : TAPS * h + 1], taps[:, TAPS * h + 1 : TAPS * h + 2]
            written_from = 0 if upper else 1
            n = QUAD - 1 if upper else QUAD
            nc.scalar.activation(
                out=stage[:, batch, first + written_from : first + QUAD, cols], in_=x[:, written_from:QUAD, :], func=ACT.Copy, scale=w_own
            )
            if upper:
                nc.scalar.activation(
                    out=last[:, batch, cols], in_=x[:, QUAD - 1, :], func=ACT.Copy, scale=carry[:, TAPS * h : TAPS * h + 1]
                )
            if on_gpsimd:
                addend = work.tile([P, QUAD + 1, HEAD], F32, tag="addend", name="addend", bufs=3)
                nc.scalar.activation(out=addend[:, 1 : 1 + n, :], in_=x[:, 0:n, :], func=ACT.Copy, scale=w_prev)
                if not upper:
                    nc.scalar.activation(out=addend[:, 0, :], in_=x[:, 0, :], func=ACT.Copy, scale=w_own)
                target = stage[:, batch, first + 1 - written_from : first + 1 + n, cols]
                nc.gpsimd.tensor_tensor(out=target, in0=target, in1=addend[:, 1 - written_from : 1 + n, :], op=ALU.add)
            else:
                later = stage[:, batch, first + 1 : first + 1 + n, cols]
                nc.vector.scalar_tensor_tensor(out=later, in0=x[:, 0:n, :], scalar=w_prev, in1=later, op0=ALU.mult, op1=ALU.add)
                if not upper:
                    slot0 = stage[:, batch, 0, cols]
                    nc.vector.scalar_tensor_tensor(out=slot0, in0=x[:, 0, :], scalar=w_own, in1=slot0, op0=ALU.mult, op1=ALU.add)

            finished = None
            if upper and h == HEADS - 1:
                for lo_row, hi_row in ((0, CARRY_SPLIT), (CARRY_SPLIT, P - 1)):
                    nc.sync.dma_start(out=stage[lo_row + 1 : hi_row + 1, batch, 0, :], in_=last[lo_row:hi_row, batch, :])
                nc.sync.dma_start(out=stage[0:1, batch, 0, :], in_=last[P - 1 : P, batch, :])
                finished = (slice(QUAD + 1, SLOTS), slice(0, BANK))
            elif unit >= UNITS - 2:
                finished = (slice(0, QUAD + 1), cols)
            elif not upper and h % 2 == 1:
                finished = (slice(0, QUAD + 1), slice((h - 1) * HEAD, (h + 1) * HEAD))
            if finished is not None:
                store = (out[batch, :, finished[0], finished[1]], stage[:, batch, finished[0], finished[1]])
                if on_gpsimd:
                    waiting.append(store)
                else:
                    nc.sync.dma_start(out=store[0], in_=store[1])

        interleave_w(nc.vector.tensor_copy, Q0, 0)
        token_tables(QUAD, QUAD + 2)
        evacuate_h(0, 0, transpose_h(0, 0))
        interleave_w(nc.vector.tensor_copy, Q0, 1)
        quantize_w(Q0, 0)
        quantize_h(0, 0, 1)
        evacuate_h(0, 1, transpose_h(0, 1))
        quantize_w(Q0, 1)
        quantize_h(0, 1, 2)
        for jj in range(2):
            evacuate_h(1, jj, transpose_h(1, jj))
        first_banks = [project_queries(tile, Q0) for tile in range(2)]
        query_products(0, Q0, first_banks[0])
        quantize_h(1, 0, 2)
        third_pair = [transpose_h(2, jj) for jj in range(2)]
        first_banks += [project_queries(tile, Q0) for tile in range(2, 4)]
        token_tables(QUAD + 2, SLOTS)
        interleave_w(nc.scalar.copy, KEYS, 0)
        for jj in range(2):
            evacuate_h(2, jj, third_pair[jj])

        load_h(4, 0, 2)
        load_w(VALUES, 0)
        load_h(5, 0, 2)
        load_w(VALUES, 1)
        nc.sync.dma_start(out=taps_v16[:], in_=conv_v.rearrange("h t -> (h t)").partition_broadcast(P))
        nc.sync.dma_start(out=taps_k16[:], in_=conv_k.rearrange("h t -> (h t)").partition_broadcast(P))

        rounds = [[(2 * pair, Q0), (2 * pair + 1, Q0)] for pair in range(PAIRS)] + [[(tile, Q1)] for tile in range(TILES)]
        w_chunks = [(KEYS, 0), (KEYS, 1), (VALUES, 0), (VALUES, 1), (Q1, 0), (Q1, 1)]
        interleave_at = {0: 1, 2: 2, 3: 3, 4: 4, 5: 5}
        quantize_at = {1: [2, 3], 2: [4], 3: [5], 4: [6], 5: [7]}
        convolve_keys_at = {KEYS_FROM + unit + (1 if unit < UNITS - 1 else 2): unit for unit in range(UNITS)}
        key_terms = {}
        for m, q_jobs in enumerate(rounds):
            k_unit, v_unit = m - KEYS_FROM, m - VALUES_FROM
            with_k = 0 <= k_unit < UNITS
            with_v = 0 <= v_unit < UNITS
            from_earlier_rounds = len(waiting)

            if with_v:
                v_bank = project_values(v_unit)
            q_banks = first_banks[2 * m : 2 * m + 2] if m < 2 else [project_queries(*job) for job in q_jobs]
            if with_k:
                k_bank = project_keys(k_unit)
            if m in convolve_keys_at:
                summed = key_sums(key_terms[convolve_keys_at[m]])
            if m + 3 < PAIRS:
                h_banks = [transpose_h(m + 3, jj) for jj in range(2)]
            if m in CHANNEL_TABLES_AT:
                table_banks = transpose_tables(CHANNEL_TABLES_AT[m])

            if m > 0:
                query_products(*q_jobs[0], q_banks[0])
            if with_v:
                on_gpsimd = v_unit % HEADS == 0 and v_unit < UNITS // 2
                convolve(v_stage, v_last, taps_v, carry_v, v_out, v_unit, v_bank, on_gpsimd)
            if m in convolve_keys_at:
                convolve(k_stage, k_last, taps_k, carry_k, k_out, convolve_keys_at[m], summed, True)
            if with_k:
                key_terms[k_unit] = key_products(k_unit, k_bank)
            for job, bank in zip(q_jobs[1:], q_banks[1:]):
                query_products(*job, bank)

            for pair in quantize_at.get(m, []):
                quantize_h(pair, 0, 2)
            if 1 <= m <= len(w_chunks):
                quantize_w(*w_chunks[m - 1])
            tile, group = q_jobs[-1]
            if m == len(rounds) - 1:
                query_sums(tile // 2, group, 0, 1, nc.vector, 1)
                query_sums(tile // 2, group, 1, 2, nc.vector, 1)
            elif tile % 2 == 1:
                query_sums(tile // 2, group, 0, 2, nc.gpsimd, 2 if m <= len(w_chunks) else 1)
            flush(from_earlier_rounds if m >= PAIRS else len(waiting))

            if m + 3 < PAIRS:
                for jj in range(2):
                    evacuate_h(m + 3, jj, h_banks[jj])
            if m in CHANNEL_TABLES_AT:
                channel_tables(CHANNEL_TABLES_AT[m], table_banks)
            if m in interleave_at:
                interleave_w(nc.scalar.copy, *w_chunks[interleave_at[m]])
            if m < PASSES:
                load_h(PAIRS - 2 + m, 0, 2)
                load_w(Q1, m)
            if m == LOWER_TABLES_AT:
                token_tables(0, QUAD)
            if m + 2 in CHANNEL_TABLES_AT:
                repeat_cosine(CHANNEL_TABLES_AT[m + 2])
            if m == KEYS_FROM - 1:
                prepare_taps()
        flush(len(waiting))
